import numpy as np
import ml_dtypes


def mxq(x, axis, fmt="e4m3"):
    dtype, down = {"e4m3": (ml_dtypes.float8_e4m3fn, 7), "e5m2": (ml_dtypes.float8_e5m2, 14)}[fmt]
    v = np.moveaxis(np.asarray(x, np.float32).astype(ml_dtypes.bfloat16).astype(np.float64), axis, -1)
    blocks = v.reshape(v.shape[:-1] + (-1, 32))
    amax = np.abs(blocks).max(-1, keepdims=True)
    byte = np.maximum(np.where(amax > 0, np.frexp(amax)[1] - 1 + 127, 0) - down, 1)
    scale = np.exp2(byte - 127.0)
    codes = (blocks / scale).astype(np.float32).astype(dtype).astype(np.float64)
    return np.moveaxis((codes * scale).reshape(v.shape), -1, axis)


WIDE = False


def mx_kscale(k):
    if not WIDE:
        return np.ones(k)
    levels = np.array([10, -10, 5, -5, 0])
    if k % 512:
        return np.exp2(np.random.permutation(np.resize(levels, k // 32))).repeat(32)
    a = np.empty((k // 512, 16))
    for p in range(k // 512):
        a[p, :8] = np.random.permutation(np.resize(levels, 8))
        for g in range(8):
            far = levels[np.abs(levels - a[p, g]) >= 10]
            a[p, g + 8] = far[np.random.randint(len(far))]
    return np.exp2(a.ravel()).repeat(32)


BF16 = ml_dtypes.bfloat16


def bf(x):
    return np.asarray(x, np.float32).astype(BF16)


def f64(x):
    return np.asarray(x).astype(np.float64)


B, DIM = 4096, 256
K = 2 * DIM


def sigmoid(v):
    return 1.0 / (1.0 + np.exp(-v))


def setup_inputs():
    s = mx_kscale(K)

    def w():
        return bf(np.random.standard_normal((DIM, K)) / np.sqrt(K) / s[None, :])

    def b():
        return bf(np.random.standard_normal(DIM) * 0.2)

    inp = {}
    inp["x"] = bf(np.random.standard_normal((B, DIM)) * s[:DIM])
    inp["h"] = bf(np.random.standard_normal((B, DIM)) * s[DIM:])
    inp["c"] = bf(np.random.standard_normal((B, DIM)))
    inp["n"] = bf(0.5 + np.random.uniform(0.0, 1.0, (B, DIM)))
    inp["m"] = bf(np.random.standard_normal((B, DIM)))
    for g in ("i", "f", "o", "z"):
        inp["W_" + g] = w()
        inp["b_" + g] = b()
    return inp


def reference(x, h, c, n, m, W_i, b_i, W_f, b_f, W_o, b_o, W_z, b_z):
    c, n, m = f64(c), f64(n), f64(m)
    combined = np.concatenate([f64(x), f64(h)], axis=-1)
    W = np.concatenate([f64(W_i), f64(W_f), f64(W_o), f64(W_z)], axis=0)
    b = np.concatenate([f64(b_i), f64(b_f), f64(b_o), f64(b_z)], axis=0)
    gates = (mxq(combined, 1, "e4m3") @ mxq(W, 1, "e4m3").T) + b
    i_t, f_t, o_t, z_t = np.split(gates, 4, axis=-1)
    z = np.tanh(z_t)
    m_new = np.maximum(f_t + m, i_t)
    i = np.exp(i_t - m_new)
    f = np.exp(f_t + m - m_new)
    c_new = f * c + i * z
    n_new = f * n + i
    h_new = sigmoid(o_t) * (c_new / (n_new + 1e-6))
    return np.stack([h_new, c_new, n_new, m_new])

@@ -1,0 +1,569 @@
+from contextlib import ExitStack
+
+import concourse.mybir as mybir
+from concourse.masks import make_identity
+
+F32 = mybir.dt.float32
+BF16 = mybir.dt.bfloat16
+U32 = mybir.dt.uint32
+U8 = mybir.dt.uint8
+FP8X4 = mybir.dt.float8_e4m3fn_x4
+ACT = mybir.ActivationFunctionType
+ALU = mybir.AluOpType
+
+P = 128
+B = 4096
+DIM = 256
+NT = B // P
+NQ = NT // 4
+PW = 2 * DIM
+QW = 4 * DIM
+EPS = 1e-6
+FLOPS = 2 * B * 2 * DIM * 4 * DIM
+
+CHUNKS = [(0, 3), (3, 6), (6, 8)]
+B_AT = {5: [0], 6: [1], 7: [2], 8: [3, 4], 9: [5, 6, 7]}
+NITER = NQ + 2
+DUP = 0
+P2_ON_GPSIMD = False
+CN_ON_GPSIMD = False
+MB_ON_GPSIMD = True
+GI, GF, GZ, GO, GN = 0, 2, 4, 6, 8
+NRING = 6
+
+
+def tile_slstmcell_t_kernel(tc, x, h, c, n, m, W_i, b_i, W_f, b_f, W_o, b_o, W_z, b_z, out):
+    nc = tc.nc
+    ln_at = {}
+    for ci, (s, e) in enumerate(CHUNKS):
+        ln_at[e] = ci
+
+    xv = x.rearrange("(p t) d -> p (t d)", t=NT)
+    hv = h.rearrange("(p t) d -> p (t d)", t=NT)
+    cv = c.rearrange("(p t) d -> p (t d)", t=NT)
+    nv = n.rearrange("(p t) d -> p (t d)", t=NT)
+    mv = m.rearrange("(p t) d -> p (t d)", t=NT)
+    ov = out.rearrange("g (p t) d -> g p (t d)", t=NT)
+
+    with ExitStack() as ctx:
+        ctx.enter_context(tc.manual_schedule())
+        const = ctx.enter_context(tc.tile_pool(name="const", bufs=1))
+        ps = ctx.enter_context(tc.psum_pool(name="ps", bufs=1))
+        ld = ctx.enter_context(tc.tile_pool(name="ld", bufs=3))
+        grp = ctx.enter_context(tc.tile_pool(name="grp", bufs=2))
+        wst = ctx.enter_context(tc.tile_pool(name="wst", bufs=1))
+        gt = ctx.enter_context(tc.tile_pool(name="gt", bufs=2))
+        wk = ctx.enter_context(tc.tile_pool(name="wk", bufs=2))
+        ost = ctx.enter_context(tc.tile_pool(name="ost", bufs=2))
+        ring = ctx.enter_context(tc.tile_pool(name="ring", bufs=6))
+
+        ident32 = const.tile([P, P], F32, name="ident32")
+        identb = const.tile([P, P], BF16, name="identb")
+        negi = const.tile([P, P], BF16, name="negi")
+        brow = const.tile([P, P], BF16, name="brow")
+        bcol = const.tile([P, 8], F32, name="bcol")
+        bhalf = const.tile([P, 2], F32, name="bhalf")
+        bd = const.tile([P, 2], F32, name="bd")
+        epsc = const.tile([P, 1], F32, name="epsc")
+        bfb = const.tile([P, DIM], BF16, name="bfb")
+        bfrow = const.tile([P, DIM], BF16, name="bfrow")
+        ones = const.tile([P, P], BF16, name="ones")
+        wc = const.tile([P, 10 * P], U32, name="wc", align_bytes=64)
+        wscl = const.tile([P, 10 * P], U8, name="wscl", align_bytes=64)
+        codes = const.tile([P, B], U32, name="codes", align_bytes=64)
+        scl = const.tile([P, B], U8, name="scl", align_bytes=64)
+        w_sb = wst.tile([P, 8 * 512], BF16, name="w_sb")
+        gw = wst.tile([P, 10 * 512], BF16, name="gw", align_bytes=64)
+
+        xhq, mq, cq, nq, mbq, gq = {}, {}, {}, {}, {}, {}
+        dT, zT, thT = {}, {}, {}
+        e1q, e2q, fnq, nnq, cnq, mnq, hhq, pq, sqq, a_t = {}, {}, {}, {}, {}, {}, {}, {}, {}, {}
+        quantised = {}
+
+        fills = []
+        state = {"filled": 0, "used": 0, "tpe": 0, "tact": 0}
+        bankof = {}
+        jobs = []
+
+        def pump():
+            while fills and state["filled"] - state["used"] < NRING:
+                if not fills[0]():
+                    break
+                fills.pop(0)
+                state["filled"] += 1
+
+        def used():
+            state["used"] += 1
+            pump()
+
+        def tpump():
+            while state["tpe"] < len(jobs) and state["tpe"] - state["tact"] < 2:
+                if not jobs[state["tpe"]][0]():
+                    break
+                state["tpe"] += 1
+
+        def tjob():
+            tpump()
+            assert state["tpe"] > state["tact"], "job not ready"
+            jobs[state["tact"]][1]()
+            state["tact"] += 1
+            tpump()
+            pump()
+
+        def load(dst, q, src, tag):
+            dst[q] = ld.tile([P, QW], BF16, name=tag + "q", tag=tag)
+            nc.sync.dma_start(out=dst[q][:], in_=src[:, q * QW : (q + 1) * QW])
+
+        def load_xh(q):
+            xhq[q] = ld.tile([P, 4 * 512], BF16, name="xhq", tag="xh")
+            for half_, src in enumerate((xv, hv)):
+                nc.sync.dma_start(
+                    out=xhq[q][:].rearrange("p (t s d) -> p t s d", t=4, s=2)[:, :, half_, :],
+                    in_=src[:, q * QW : (q + 1) * QW].rearrange("p (t d) -> p t d", t=4),
+                )
+
+        def store(g, q, t):
+            nc.sync.dma_start(out=ov[g, :, q * QW : (q + 1) * QW], in_=t[:])
+
+        tb_of = {}
+
+        def add_e1(key, ins_fn, out_fn, eng, ready_fn):
+            def pe():
+                if not ready_fn():
+                    return False
+                tp = ps.tile([P, 512], F32, name="bank_T", tag="T", bufs=2)
+                tb_of[key] = tp
+                for i, src in enumerate(ins_fn()):
+                    nc.tensor.transpose(tp[:, i * P : (i + 1) * P], src, ident32[:])
+                return True
+
+            def drain():
+                src = tb_of[key][:].rearrange("p (s u c) -> p s c u", s=2, u=2)
+                if eng == "act":
+                    nc.scalar.copy(out=out_fn(), in_=src)
+                else:
+                    nc.vector.tensor_copy(out=out_fn(), in_=src)
+
+            jobs.append((pe, drain))
+
+        def add_e1_w(k, eng):
+            w32 = w_sb[:].bitcast(F32)
+            gw32 = gw[:, 0 : 8 * 512].bitcast(F32).rearrange("p (s c u) -> p s c u", s=8, u=2)
+            add_e1(
+                ("w", k),
+                lambda: [w32[:, (2 * k + s) * 256 + u : (2 * k + s + 1) * 256 : 2] for s in range(2) for u in range(2)],
+                lambda: gw32[:, 2 * k : 2 * k + 2],
+                eng,
+                lambda: True,
+            )
+
+        def add_e1_pair(j, eng):
+            q, jj = j // 2, j % 2
+
+            def ins():
+                xh32 = xhq[q][:].bitcast(F32)
+                res = []
+                for tt in range(2):
+                    t = 2 * jj + tt
+                    for u in range(2):
+                        res.append(xh32[:, t * 256 + u : (t + 1) * 256 : 2])
+                return res
+
+            def dst():
+                if jj == 0:
+                    gq[q] = grp.tile([P, 4 * 512], BF16, name="g", tag="g", align_bytes=64)
+                g32 = gq[q][:].bitcast(F32).rearrange("p (t c u) -> p t c u", t=4, u=2)
+                return g32[:, 2 * jj : 2 * jj + 2]
+
+            add_e1(("x", j), ins, dst, eng, lambda: q in xhq)
+            if jj == 1 and q + 3 < NQ:
+                pe_, drain_ = jobs.pop()
+
+                def drain_and_load():
+                    drain_()
+                    load_xh(q + 3)
+
+                jobs.append((pe_, drain_and_load))
+
+        def add_exit(q, blk, dst, func, bias, scale, tag, bufs, blk2=None):
+            key = (tag, q, blk)
+
+            def pe():
+                if q not in quantised or blk not in quantised_w or (blk2 is not None and blk2 not in quantised_w):
+                    return False
+                tbk = ps.tile([P, 512], F32, name="bank_T", tag="T", bufs=2)
+                tb_of[key] = tbk
+                seq = [(blk, True, True)] * DUP
+                if blk2 is None:
+                    seq.append((blk, True, True))
+                else:
+                    seq.append((blk, True, False))
+                    seq.append((blk2, False, True))
+                for bl, st, sp in seq:
+                    nc.tensor.matmul_mx(
+                        out=tbk[:],
+                        lhsT=wc[:, bl * P : (bl + 1) * P].bitcast(FP8X4),
+                        lhsT_scale=wscl[:, bl * P : (bl + 1) * P],
+                        rhs=codes[:, q * 512 : (q + 1) * 512].bitcast(FP8X4),
+                        rhs_scale=scl[:, q * 512 : (q + 1) * 512],
+                        start=st,
+                        stop=sp,
+                    )
+                return True
+
+            def drain():
+                dst[(q, blk % 2)] = gt.tile([P, 512], F32, name=tag, tag=tag + str(blk % 2), bufs=bufs)
+                nc.scalar.activation(out=dst[(q, blk % 2)][:], in_=tb_of[key][:], func=func, bias=bias, scale=scale)
+
+            jobs.append((pe, drain))
+
+        quantised_w = {}
+
+        def add_exit_d(q):
+            for r in range(2):
+                add_exit(q, GI + r, dT, ACT.Identity, bd[:, r : r + 1], 1.0, "dT", 2, blk2=GN + r)
+
+        def add_exit_z(q):
+            for r in range(2):
+                add_exit(q, GZ + r, zT, ACT.Tanh, bcol[:, GZ + r : GZ + r + 1], 1.0, "zT", 2)
+
+        def add_exit_o(q):
+            for r in range(2):
+                add_exit(q, GO + r, thT, ACT.Tanh, bhalf[:, r : r + 1], 0.5, "thT", 3)
+
+        def quant(q):
+            nc.vector.quantize_mx(
+                out=codes[:, q * 512 : (q + 1) * 512].bitcast(FP8X4),
+                scales=scl[:, q * 512 : (q + 1) * 512],
+                in_=gq[q][:],
+            )
+            quantised[q] = True
+            tpump()
+            pump()
+
+        def quant_w(s0, nblk):
+            nc.vector.quantize_mx(
+                out=wc[:, s0 * P : (s0 + nblk) * P].bitcast(FP8X4),
+                scales=wscl[:, s0 * P : (s0 + nblk) * P],
+                in_=gw[:, s0 * 512 : (s0 + nblk) * 512],
+            )
+            for bl in range(s0, s0 + nblk):
+                quantised_w[bl] = True
+            tpump()
+            pump()
+
+        def new_bank(key):
+            bankof[key] = ps.tile([P, 512], F32, name="bank_B", tag="B", bufs=NRING)
+            return bankof[key]
+
+        def add_f(j):
+            def go():
+                if j // 2 not in quantised or GF not in quantised_w:
+                    return False
+                bk = new_bank(("F", j))
+                for tt in range(2):
+                    t = 2 * j + tt
+                    nc.tensor.matmul_mx(
+                        out=bk[:, tt * DIM : (tt + 1) * DIM],
+                        lhsT=codes[:, t * P : (t + 1) * P].bitcast(FP8X4),
+                        lhsT_scale=scl[:, t * P : (t + 1) * P],
+                        rhs=wc[:, GF * P : (GF + 2) * P].bitcast(FP8X4),
+                        rhs_scale=wscl[:, GF * P : (GF + 2) * P],
+                        start=True,
+                        stop=True,
+                    )
+                return True
+
+            fills.append(go)
+
+        def add_back(kind, src, j, minus_m):
+            q, jj = j // 2, j % 2
+
+            def go():
+                if (q, 0) not in src or (q, 1) not in src:
+                    return False
+                bk = new_bank((kind, j))
+                if minus_m:
+                    nc.tensor.matmul(out=bk[:], lhsT=negi[:], rhs=mq[q][:, jj * PW : (jj + 1) * PW], start=True, stop=False)
+                for tt in range(2):
+                    for r in range(2):
+                        o = bk[:, tt * DIM + r * P : tt * DIM + (r + 1) * P]
+                        i = src[(q, r)][:, (2 * jj + tt) * P : (2 * jj + tt + 1) * P]
+                        if minus_m:
+                            nc.tensor.matmul(out=o, lhsT=i, rhs=ident32[:], is_transpose=True, start=False, stop=(tt == 1 and r == 1))
+                        else:
+                            nc.tensor.transpose(o, i, ident32[:])
+                return True
+
+            fills.append(go)
+
+        def half(t, j):
+            return t[:, (j % 2) * PW : (j % 2 + 1) * PW]
+
+        def mb(q, eng):
+            mbq[q] = wk.tile([P, QW], F32, name="mb", tag="mb")
+            for t in range(4):
+                cols = slice(t * DIM, (t + 1) * DIM)
+                eng.tensor_tensor(out=mbq[q][:, cols], in0=mq[q][:, cols], in1=bfb[:], op=ALU.add)
+
+        def v_a(j):
+            a_t[j] = wk.tile([P, PW], F32, name="a", tag="a")
+            nc.vector.tensor_tensor(out=a_t[j][:], in0=bankof[("F", j)][:], in1=half(mbq[j // 2], j), op=ALU.add)
+            used()
+
+        def v_mn(j):
+            q = j // 2
+            if j % 2 == 0:
+                mnq[q] = ost.tile([P, QW], F32, name="mn", tag="mn")
+                e1q[q] = wk.tile([P, QW], F32, name="e1", tag="e1")
+                e2q[q] = wk.tile([P, QW], F32, name="e2", tag="e2")
+            d = bankof[("D", j)]
+            nc.vector.scalar_tensor_tensor(out=half(mnq[q], j), in0=d[:], scalar=0.0, in1=a_t[j][:], op0=ALU.max, op1=ALU.add)
+            nc.scalar.activation(out=half(e1q[q], j), in_=d[:], func=ACT.Exp, scale=1.0)
+            nc.scalar.activation(out=half(e2q[q], j), in_=d[:], func=ACT.Exp, scale=-1.0)
+            used()
+            if j % 2 == 1:
+                store(3, q, mnq[q])
+
+        def v_fn(q):
+            fnq[q] = wk.tile([P, QW], F32, name="fn", tag="fn")
+            nc.vector.scalar_tensor_tensor(out=fnq[q][:], in0=e2q[q][:], scalar=1.0, in1=nq[q][:], op0=ALU.min, op1=ALU.mult)
+
+        def v_nn(q):
+            nnq[q] = ost.tile([P, QW], F32, name="nn", tag="nn", bufs=3 if CN_ON_GPSIMD else 2)
+            nc.vector.scalar_tensor_tensor(out=nnq[q][:], in0=e1q[q][:], scalar=1.0, in1=fnq[q][:], op0=ALU.min, op1=ALU.add)
+            store(2, q, nnq[q])
+            sqq[q] = ring.tile([P, QW], F32, name="sq", tag="sq")
+            nc.scalar.activation(out=sqq[q][:], in_=nnq[q][:], func=ACT.Square, bias=epsc[:], scale=1.0)
+
+        def v_fc(q):
+            nc.vector.scalar_tensor_tensor(out=e2q[q][:], in0=e2q[q][:], scalar=1.0, in1=cq[q][:], op0=ALU.min, op1=ALU.mult)
+
+        def v_iz(j):
+            e1h = half(e1q[j // 2], j)
+            nc.vector.scalar_tensor_tensor(out=e1h, in0=e1h, scalar=1.0, in1=bankof[("Z", j)][:], op0=ALU.min, op1=ALU.mult)
+            used()
+
+        def v_cn(q):
+            cnq[q] = ost.tile([P, QW], F32, name="cn", tag="cn", bufs=3 if CN_ON_GPSIMD else 2)
+            if CN_ON_GPSIMD:
+                for t in range(4):
+                    cols = slice(t * DIM, (t + 1) * DIM)
+                    nc.gpsimd.tensor_tensor(out=cnq[q][:, cols], in0=e1q[q][:, cols], in1=e2q[q][:, cols], op=ALU.add)
+            else:
+                nc.vector.tensor_tensor(out=cnq[q][:], in0=e1q[q][:], in1=e2q[q][:], op=ALU.add)
+            store(1, q, cnq[q])
+
+        r2done, p2done = {}, {}
+
+        def g_p2(q):
+            if P2_ON_GPSIMD and q in pq and q in r2done and q not in p2done:
+                p2done[q] = True
+                for t in range(4):
+                    cols = slice(t * DIM, (t + 1) * DIM)
+                    nc.gpsimd.tensor_tensor(out=sqq[q][:, cols], in0=pq[q][:, cols], in1=sqq[q][:, cols], op=ALU.mult)
+
+        def v_p(q):
+            pq[q] = ring.tile([P, QW], F32, name="p", tag="p")
+            nc.vector.scalar_tensor_tensor(out=pq[q][:], in0=nnq[q][:], scalar=EPS, in1=cnq[q][:], op0=ALU.add, op1=ALU.mult)
+            g_p2(q)
+
+        def s_ln(ci):
+            for q in range(CHUNKS[ci][0], CHUNKS[ci][1]):
+                nc.scalar.activation(out=sqq[q][:], in_=sqq[q][:], func=ACT.Ln, scale=2.0)
+
+        def s_r2(q):
+            nc.scalar.activation(out=sqq[q][:], in_=sqq[q][:], func=ACT.Exp, scale=-1.0)
+            r2done[q] = True
+            g_p2(q)
+
+        def v_p2(q):
+            if not P2_ON_GPSIMD:
+                nc.vector.tensor_tensor(out=sqq[q][:], in0=pq[q][:], in1=sqq[q][:], op=ALU.mult)
+
+        def v_h(j):
+            q = j // 2
+            if j % 2 == 0:
+                hhq[q] = ost.tile([P, QW], F32, name="hh", tag="hh")
+            nc.vector.scalar_tensor_tensor(out=half(hhq[q], j), in0=bankof[("TH", j)][:], scalar=1.0, in1=half(sqq[q], j), op0=ALU.add, op1=ALU.mult)
+            used()
+            if j % 2 == 1:
+                store(0, q, hhq[q])
+
+        add_e1_w(0, "act")
+        add_e1_w(1, "dve")
+        add_e1_pair(0, "act")
+        add_e1_pair(1, "dve")
+        add_exit_d(0)
+        add_e1_pair(2, "dve")
+        add_e1_pair(3, "dve")
+        add_e1_w(2, "act")
+        add_e1_pair(4, "dve")
+        add_e1_pair(5, "dve")
+        per_it = {}
+        for it in range(NITER):
+            n0 = len(jobs)
+            if it + 1 < NQ:
+                add_exit_d(it + 1)
+            if it < NQ:
+                add_exit_z(it)
+            for bq in B_AT.get(it + 1, []):
+                add_exit_o(bq)
+            if it + 3 < NQ:
+                add_e1_pair(2 * (it + 3), "act")
+                add_e1_pair(2 * (it + 3) + 1, "act")
+            if it == 0:
+                add_e1_w(3, "act")
+            per_it[it] = len(jobs) - n0
+        for it in range(NITER):
+            if it < NQ:
+                add_f(2 * it)
+                add_f(2 * it + 1)
+                add_back("D", dT, 2 * it, True)
+                add_back("D", dT, 2 * it + 1, True)
+            if 1 <= it <= NQ:
+                add_back("Z", zT, 2 * (it - 1), False)
+                add_back("Z", zT, 2 * (it - 1) + 1, False)
+            for bq in B_AT.get(it, []):
+                add_back("TH", thT, 2 * bq, False)
+                add_back("TH", thT, 2 * bq + 1, False)
+
+        make_identity(nc, ident32[:])
+        nc.vector.memset(brow[:], 0.0)
+        nc.vector.memset(epsc[:], EPS)
+        nc.vector.memset(bfrow[:], 0.0)
+        nc.vector.memset(ones[:], 1.0)
+        nc.scalar.dma_start(out=brow[0:2, :], in_=b_i.rearrange("(r c) -> r c", r=2))
+        nc.scalar.dma_start(out=brow[2:4, :], in_=b_f.rearrange("(r c) -> r c", r=2))
+        nc.scalar.dma_start(out=bfrow[0:1, :], in_=b_f.rearrange("(r c) -> r c", r=1))
+        nc.scalar.dma_start(out=brow[4:6, :], in_=b_z.rearrange("(r c) -> r c", r=2))
+        nc.scalar.dma_start(out=brow[6:8, :], in_=b_o.rearrange("(r c) -> r c", r=2))
+
+        def load_w(s0, wg):
+            nc.sync.dma_start(
+                out=w_sb[:, s0 * 512 : (s0 + 2) * 512].rearrange("p (r k) -> p r k", r=2),
+                in_=wg.rearrange("(r p) k -> p r k", p=P),
+            )
+
+        load_w(GI, W_i)
+        load_w(GF, W_f)
+        load_xh(0)
+        load(mq, 0, mv, "m")
+        load_xh(1)
+        load_w(GZ, W_z)
+        load_xh(2)
+        load(cq, 0, cv, "c")
+        load(nq, 0, nv, "n")
+        load(mq, 1, mv, "m")
+        load_w(GO, W_o)
+
+        nc.vector.tensor_copy(out=identb[:], in_=ident32[:])
+        nc.vector.tensor_scalar(out=negi[:], in0=ident32[:], scalar1=-1.0, scalar2=None, op0=ALU.mult)
+        tjob()
+        tjob()
+        nc.vector.tensor_scalar(out=gw[:, GN * 512 : (GN + 2) * 512], in0=gw[:, GF * 512 : (GF + 2) * 512], scalar1=-1.0, scalar2=None, op0=ALU.mult)
+        quant_w(GI, 4)
+        tjob()
+        tjob()
+        tb = ps.tile([P, 512], F32, name="bank_B", tag="B", bufs=NRING)
+        tbb = tb[:].bitcast(BF16)
+        nc.tensor.transpose(tbb[:, 0:P], brow[:], identb[:])
+        nc.vector.tensor_copy(out=bcol[:], in_=tbb[:, 0:8])
+        nc.tensor.matmul(out=tb[:, DIM : 2 * DIM], lhsT=ones[:], rhs=bfrow[:], start=True, stop=True)
+        nc.vector.tensor_copy(out=bfb[:], in_=tb[:, DIM : 2 * DIM])
+        nc.vector.tensor_scalar(out=bhalf[:], in0=bcol[:, GO : GO + 2], scalar1=0.5, scalar2=None, op0=ALU.mult)
+        nc.vector.tensor_tensor(out=bd[:], in0=bcol[:, GI : GI + 2], in1=bcol[:, GF : GF + 2], op=ALU.subtract)
+        state["filled"] += 1
+        state["used"] += 1
+
+        quant_w(GN, 2)
+        quant(0)
+        mb(0, nc.vector)
+        tjob()
+        tjob()
+        pump()
+
+        def startup(it, pos):
+            if it == 0 and pos == 0:
+                tjob()
+                tjob()
+                tjob()
+                tjob()
+                tjob()
+            if it == 0 and pos == 1:
+                quant(1)
+                quant_w(GZ, 2)
+                quant(2)
+            if it == 1 and pos == 3:
+                quant_w(GO, 2)
+
+        for it in range(NITER):
+            qa = it if it < NQ else None
+            qk = it - 1 if 1 <= it <= NQ else None
+            bs = B_AT.get(it, [])
+            b0 = bs[0] if bs else None
+            todo = per_it[it]
+            if it + 2 < NQ:
+                load(mq, it + 2, mv, "m")
+            if it + 1 < NQ:
+                load(cq, it + 1, cv, "c")
+                load(nq, it + 1, nv, "n")
+
+            def act_jobs(k):
+                for z_ in range(k):
+                    tjob()
+
+            if it + 1 < NQ:
+                mb(it + 1, nc.gpsimd if MB_ON_GPSIMD else nc.vector)
+            first = min(4, todo) if it > 0 else 0
+            act_jobs(first)
+            todo -= first
+            if qa is not None:
+                v_a(2 * qa)
+                v_a(2 * qa + 1)
+            if CN_ON_GPSIMD and 2 <= it <= NQ + 1:
+                v_p(it - 2)
+            if qk is not None:
+                v_fn(qk)
+            if qa is not None:
+                v_mn(2 * qa)
+            if qk is not None:
+                v_nn(qk)
+            startup(it, 0)
+            if qk is not None:
+                v_fc(qk)
+            if qa is not None:
+                v_mn(2 * qa + 1)
+            startup(it, 1)
+            startup(it, 2)
+            if qk is not None:
+                v_iz(2 * qk)
+            if b0 is not None:
+                v_p2(b0)
+            if qk is not None:
+                v_iz(2 * qk + 1)
+            if b0 is not None:
+                v_h(2 * b0)
+            if qk is not None:
+                v_cn(qk)
+            if b0 is not None:
+                v_h(2 * b0 + 1)
+            if qk is not None and not CN_ON_GPSIMD:
+                v_p(qk)
+            startup(it, 3)
+            act_jobs(todo)
+            fresh = range(CHUNKS[ln_at[it]][0], CHUNKS[ln_at[it]][1]) if it in ln_at else []
+            for bq in B_AT.get(it + 1, []):
+                if bq not in fresh:
+                    s_r2(bq)
+            if it in ln_at:
+                s_ln(ln_at[it])
+            for bq in B_AT.get(it + 1, []):
+                if bq in fresh:
+                    s_r2(bq)
+            for bq in bs[1:]:
+                v_p2(bq)
+                v_h(2 * bq)
+                v_h(2 * bq + 1)
+            if 3 <= it + 2 < NQ:
+                quant(it + 2)

@@ -27,7 +27,6 @@ NITER = NQ + 2
 DUP = 0
 P2_ON_GPSIMD = False
 CN_ON_GPSIMD = False
-MB_ON_GPSIMD = True
 GI, GF, GZ, GO, GN = 0, 2, 4, 6, 8
 NRING = 6
 
@@ -59,14 +58,13 @@ def tile_slstmcell_t_kernel(tc, x, h, c, n, m, W_i, b_i, W_f, b_f, W_o, b_o, W_z
 
         ident32 = const.tile([P, P], F32, name="ident32")
         identb = const.tile([P, P], BF16, name="identb")
-        negi = const.tile([P, P], BF16, name="negi")
         brow = const.tile([P, P], BF16, name="brow")
         bcol = const.tile([P, 8], F32, name="bcol")
         bhalf = const.tile([P, 2], F32, name="bhalf")
         bd = const.tile([P, 2], F32, name="bd")
         epsc = const.tile([P, 1], F32, name="epsc")
-        bfb = const.tile([P, DIM], BF16, name="bfb")
-        bfrow = const.tile([P, DIM], BF16, name="bfrow")
+        bib = const.tile([P, PW], BF16, name="bib")
+        birow = const.tile([P, DIM], BF16, name="birow")
         ones = const.tile([P, P], BF16, name="ones")
         wc = const.tile([P, 10 * P], U32, name="wc", align_bytes=64)
         wscl = const.tile([P, 10 * P], U8, name="wscl", align_bytes=64)
@@ -75,7 +73,7 @@ def tile_slstmcell_t_kernel(tc, x, h, c, n, m, W_i, b_i, W_f, b_f, W_o, b_o, W_z
         w_sb = wst.tile([P, 8 * 512], BF16, name="w_sb")
         gw = wst.tile([P, 10 * 512], BF16, name="gw", align_bytes=64)
 
-        xhq, mq, cq, nq, mbq, gq = {}, {}, {}, {}, {}, {}
+        xhq, mq, cq, nq, gq = {}, {}, {}, {}, {}
         dT, zT, thT = {}, {}, {}
         e1q, e2q, fnq, nnq, cnq, mnq, hhq, pq, sqq, a_t = {}, {}, {}, {}, {}, {}, {}, {}, {}, {}
         quantised = {}
@@ -221,7 +219,7 @@ def tile_slstmcell_t_kernel(tc, x, h, c, n, m, W_i, b_i, W_f, b_f, W_o, b_o, W_z
 
         def add_exit_d(q):
             for r in range(2):
-                add_exit(q, GI + r, dT, ACT.Identity, bd[:, r : r + 1], 1.0, "dT", 2, blk2=GN + r)
+                add_exit(q, GF + r, dT, ACT.Identity, bd[:, r : r + 1], 1.0, "dT", 2, blk2=GN + r)
 
         def add_exit_z(q):
             for r in range(2):
@@ -256,19 +254,19 @@ def tile_slstmcell_t_kernel(tc, x, h, c, n, m, W_i, b_i, W_f, b_f, W_o, b_o, W_z
             bankof[key] = ps.tile([P, 512], F32, name="bank_B", tag="B", bufs=NRING)
             return bankof[key]
 
-        def add_f(j):
+        def add_i(j):
             def go():
-                if j // 2 not in quantised or GF not in quantised_w:
+                if j // 2 not in quantised or GI not in quantised_w:
                     return False
-                bk = new_bank(("F", j))
+                bk = new_bank(("I", j))
                 for tt in range(2):
                     t = 2 * j + tt
                     nc.tensor.matmul_mx(
                         out=bk[:, tt * DIM : (tt + 1) * DIM],
                         lhsT=codes[:, t * P : (t + 1) * P].bitcast(FP8X4),
                         lhsT_scale=scl[:, t * P : (t + 1) * P],
-                        rhs=wc[:, GF * P : (GF + 2) * P].bitcast(FP8X4),
-                        rhs_scale=wscl[:, GF * P : (GF + 2) * P],
+                        rhs=wc[:, GI * P : (GI + 2) * P].bitcast(FP8X4),
+                        rhs_scale=wscl[:, GI * P : (GI + 2) * P],
                         start=True,
                         stop=True,
                     )
@@ -276,20 +274,20 @@ def tile_slstmcell_t_kernel(tc, x, h, c, n, m, W_i, b_i, W_f, b_f, W_o, b_o, W_z
 
             fills.append(go)
 
-        def add_back(kind, src, j, minus_m):
+        def add_back(kind, src, j, plus_m):
             q, jj = j // 2, j % 2
 
             def go():
                 if (q, 0) not in src or (q, 1) not in src:
                     return False
                 bk = new_bank((kind, j))
-                if minus_m:
-                    nc.tensor.matmul(out=bk[:], lhsT=negi[:], rhs=mq[q][:, jj * PW : (jj + 1) * PW], start=True, stop=False)
+                if plus_m:
+                    nc.tensor.matmul(out=bk[:], lhsT=identb[:], rhs=mq[q][:, jj * PW : (jj + 1) * PW], start=True, stop=False)
                 for tt in range(2):
                     for r in range(2):
                         o = bk[:, tt * DIM + r * P : tt * DIM + (r + 1) * P]
                         i = src[(q, r)][:, (2 * jj + tt) * P : (2 * jj + tt + 1) * P]
-                        if minus_m:
+                        if plus_m:
                             nc.tensor.matmul(out=o, lhsT=i, rhs=ident32[:], is_transpose=True, start=False, stop=(tt == 1 and r == 1))
                         else:
                             nc.tensor.transpose(o, i, ident32[:])
@@ -300,15 +298,9 @@ def tile_slstmcell_t_kernel(tc, x, h, c, n, m, W_i, b_i, W_f, b_f, W_o, b_o, W_z
         def half(t, j):
             return t[:, (j % 2) * PW : (j % 2 + 1) * PW]
 
-        def mb(q, eng):
-            mbq[q] = wk.tile([P, QW], F32, name="mb", tag="mb")
-            for t in range(4):
-                cols = slice(t * DIM, (t + 1) * DIM)
-                eng.tensor_tensor(out=mbq[q][:, cols], in0=mq[q][:, cols], in1=bfb[:], op=ALU.add)
-
         def v_a(j):
             a_t[j] = wk.tile([P, PW], F32, name="a", tag="a")
-            nc.vector.tensor_tensor(out=a_t[j][:], in0=bankof[("F", j)][:], in1=half(mbq[j // 2], j), op=ALU.add)
+            nc.vector.tensor_tensor(out=a_t[j][:], in0=bankof[("I", j)][:], in1=bib[:], op=ALU.add)
             used()
 
         def v_mn(j):
@@ -319,8 +311,8 @@ def tile_slstmcell_t_kernel(tc, x, h, c, n, m, W_i, b_i, W_f, b_f, W_o, b_o, W_z
                 e2q[q] = wk.tile([P, QW], F32, name="e2", tag="e2")
             d = bankof[("D", j)]
             nc.vector.scalar_tensor_tensor(out=half(mnq[q], j), in0=d[:], scalar=0.0, in1=a_t[j][:], op0=ALU.max, op1=ALU.add)
-            nc.scalar.activation(out=half(e1q[q], j), in_=d[:], func=ACT.Exp, scale=1.0)
-            nc.scalar.activation(out=half(e2q[q], j), in_=d[:], func=ACT.Exp, scale=-1.0)
+            nc.scalar.activation(out=half(e1q[q], j), in_=d[:], func=ACT.Exp, scale=-1.0)
+            nc.scalar.activation(out=half(e2q[q], j), in_=d[:], func=ACT.Exp, scale=1.0)
             used()
             if j % 2 == 1:
                 store(3, q, mnq[q])
@@ -417,8 +409,8 @@ def tile_slstmcell_t_kernel(tc, x, h, c, n, m, W_i, b_i, W_f, b_f, W_o, b_o, W_z
             per_it[it] = len(jobs) - n0
         for it in range(NITER):
             if it < NQ:
-                add_f(2 * it)
-                add_f(2 * it + 1)
+                add_i(2 * it)
+                add_i(2 * it + 1)
                 add_back("D", dT, 2 * it, True)
                 add_back("D", dT, 2 * it + 1, True)
             if 1 <= it <= NQ:
@@ -431,11 +423,11 @@ def tile_slstmcell_t_kernel(tc, x, h, c, n, m, W_i, b_i, W_f, b_f, W_o, b_o, W_z
         make_identity(nc, ident32[:])
         nc.vector.memset(brow[:], 0.0)
         nc.vector.memset(epsc[:], EPS)
-        nc.vector.memset(bfrow[:], 0.0)
+        nc.vector.memset(birow[:], 0.0)
         nc.vector.memset(ones[:], 1.0)
         nc.scalar.dma_start(out=brow[0:2, :], in_=b_i.rearrange("(r c) -> r c", r=2))
         nc.scalar.dma_start(out=brow[2:4, :], in_=b_f.rearrange("(r c) -> r c", r=2))
-        nc.scalar.dma_start(out=bfrow[0:1, :], in_=b_f.rearrange("(r c) -> r c", r=1))
+        nc.scalar.dma_start(out=birow[0:1, :], in_=b_i.rearrange("(r c) -> r c", r=1))
         nc.scalar.dma_start(out=brow[4:6, :], in_=b_z.rearrange("(r c) -> r c", r=2))
         nc.scalar.dma_start(out=brow[6:8, :], in_=b_o.rearrange("(r c) -> r c", r=2))
 
@@ -458,10 +450,9 @@ def tile_slstmcell_t_kernel(tc, x, h, c, n, m, W_i, b_i, W_f, b_f, W_o, b_o, W_z
         load_w(GO, W_o)
 
         nc.vector.tensor_copy(out=identb[:], in_=ident32[:])
-        nc.vector.tensor_scalar(out=negi[:], in0=ident32[:], scalar1=-1.0, scalar2=None, op0=ALU.mult)
         tjob()
         tjob()
-        nc.vector.tensor_scalar(out=gw[:, GN * 512 : (GN + 2) * 512], in0=gw[:, GF * 512 : (GF + 2) * 512], scalar1=-1.0, scalar2=None, op0=ALU.mult)
+        nc.vector.tensor_scalar(out=gw[:, GN * 512 : (GN + 2) * 512], in0=gw[:, GI * 512 : (GI + 2) * 512], scalar1=-1.0, scalar2=None, op0=ALU.mult)
         quant_w(GI, 4)
         tjob()
         tjob()
@@ -469,16 +460,16 @@ def tile_slstmcell_t_kernel(tc, x, h, c, n, m, W_i, b_i, W_f, b_f, W_o, b_o, W_z
         tbb = tb[:].bitcast(BF16)
         nc.tensor.transpose(tbb[:, 0:P], brow[:], identb[:])
         nc.vector.tensor_copy(out=bcol[:], in_=tbb[:, 0:8])
-        nc.tensor.matmul(out=tb[:, DIM : 2 * DIM], lhsT=ones[:], rhs=bfrow[:], start=True, stop=True)
-        nc.vector.tensor_copy(out=bfb[:], in_=tb[:, DIM : 2 * DIM])
+        nc.tensor.matmul(out=tb[:, DIM : 2 * DIM], lhsT=ones[:], rhs=birow[:], start=True, stop=True)
+        for r in range(2):
+            nc.vector.tensor_copy(out=bib[:, r * DIM : (r + 1) * DIM], in_=tb[:, DIM : 2 * DIM])
         nc.vector.tensor_scalar(out=bhalf[:], in0=bcol[:, GO : GO + 2], scalar1=0.5, scalar2=None, op0=ALU.mult)
-        nc.vector.tensor_tensor(out=bd[:], in0=bcol[:, GI : GI + 2], in1=bcol[:, GF : GF + 2], op=ALU.subtract)
+        nc.vector.tensor_tensor(out=bd[:], in0=bcol[:, GF : GF + 2], in1=bcol[:, GI : GI + 2], op=ALU.subtract)
         state["filled"] += 1
         state["used"] += 1
 
         quant_w(GN, 2)
         quant(0)
-        mb(0, nc.vector)
         tjob()
         tjob()
         pump()
@@ -513,8 +504,6 @@ def tile_slstmcell_t_kernel(tc, x, h, c, n, m, W_i, b_i, W_f, b_f, W_o, b_o, W_z
                 for z_ in range(k):
                     tjob()
 
-            if it + 1 < NQ:
-                mb(it + 1, nc.gpsimd if MB_ON_GPSIMD else nc.vector)
             first = min(4, todo) if it > 0 else 0
             act_jobs(first)
             todo -= first

@@ -21,22 +21,21 @@ QW = 4 * DIM
 EPS = 1e-6
 FLOPS = 2 * B * 2 * DIM * 4 * DIM
 
-CHUNKS = [(0, 3), (3, 6), (6, 8)]
-B_AT = {5: [0], 6: [1], 7: [2], 8: [3, 4], 9: [5, 6, 7]}
+LN_AT = {4: [0, 1, 2, 3], 7: [4, 5, 6]}
+R2_AT = {4: [0], 5: [1, 2], 6: [3]}
+O_AT = {3: [0], 4: [1], 5: [2], 6: [3, 4], 7: [5, 6, 7]}
+P2_AT = {5: [0], 6: [1, 2], 7: [3]}
+H_AT = {6: [0], 7: [1, 2], 8: [3]}
+P2_GPSIMD = [0, 1, 2, 3]
+CN_GPSIMD = [0, 1, 2, 3, 4, 5, 6]
+X_SCALAR = [6, 7, 8, 9, 10, 11, 12, 13, 14, 15]
 NITER = NQ + 2
-DUP = 0
-P2_ON_GPSIMD = False
-CN_ON_GPSIMD = False
-GI, GF, GZ, GO, GN = 0, 2, 4, 6, 8
-NRING = 6
+GI, GF, GN, GZ, GO = 0, 2, 4, 6, 8
+NRING = 4
 
 
 def tile_slstmcell_t_kernel(tc, x, h, c, n, m, W_i, b_i, W_f, b_f, W_o, b_o, W_z, b_z, out):
     nc = tc.nc
-    ln_at = {}
-    for ci, (s, e) in enumerate(CHUNKS):
-        ln_at[e] = ci
-
     xv = x.rearrange("(p t) d -> p (t d)", t=NT)
     hv = h.rearrange("(p t) d -> p (t d)", t=NT)
     cv = c.rearrange("(p t) d -> p (t d)", t=NT)
@@ -50,16 +49,16 @@ def tile_slstmcell_t_kernel(tc, x, h, c, n, m, W_i, b_i, W_f, b_f, W_o, b_o, W_z
         ps = ctx.enter_context(tc.psum_pool(name="ps", bufs=1))
         ld = ctx.enter_context(tc.tile_pool(name="ld", bufs=3))
         grp = ctx.enter_context(tc.tile_pool(name="grp", bufs=2))
-        wst = ctx.enter_context(tc.tile_pool(name="wst", bufs=1))
         gt = ctx.enter_context(tc.tile_pool(name="gt", bufs=2))
         wk = ctx.enter_context(tc.tile_pool(name="wk", bufs=2))
         ost = ctx.enter_context(tc.tile_pool(name="ost", bufs=2))
-        ring = ctx.enter_context(tc.tile_pool(name="ring", bufs=6))
+        wst = ctx.enter_context(tc.tile_pool(name="wst", bufs=1))
+        ring = ctx.enter_context(tc.tile_pool(name="ring", bufs=7))
 
         ident32 = const.tile([P, P], F32, name="ident32")
         identb = const.tile([P, P], BF16, name="identb")
         brow = const.tile([P, P], BF16, name="brow")
-        bcol = const.tile([P, 8], F32, name="bcol")
+        bcol = const.tile([P, 10], F32, name="bcol")
         bhalf = const.tile([P, 2], F32, name="bhalf")
         bd = const.tile([P, 2], F32, name="bd")
         epsc = const.tile([P, 1], F32, name="epsc")
@@ -70,37 +69,38 @@ def tile_slstmcell_t_kernel(tc, x, h, c, n, m, W_i, b_i, W_f, b_f, W_o, b_o, W_z
         wscl = const.tile([P, 10 * P], U8, name="wscl", align_bytes=64)
         codes = const.tile([P, B], U32, name="codes", align_bytes=64)
         scl = const.tile([P, B], U8, name="scl", align_bytes=64)
+        dummy = const.tile([P, 1], F32, name="dummy")
         w_sb = wst.tile([P, 8 * 512], BF16, name="w_sb")
         gw = wst.tile([P, 10 * 512], BF16, name="gw", align_bytes=64)
 
-        xhq, mq, cq, nq, gq = {}, {}, {}, {}, {}
-        dT, zT, thT = {}, {}, {}
-        e1q, e2q, fnq, nnq, cnq, mnq, hhq, pq, sqq, a_t = {}, {}, {}, {}, {}, {}, {}, {}, {}, {}
-        quantised = {}
+        xhq, mq, ncq, gq = {}, {}, {}, {}
+        eT, zT, thT = {}, {}, {}
+        e1q, e2q, fq, nnq, cnq, mnq, hhq, pq, sqq, a_t = {}, {}, {}, {}, {}, {}, {}, {}, {}, {}
+        quantised, quantised_w = {}, {}
 
-        fills = []
-        state = {"filled": 0, "used": 0, "tpe": 0, "tact": 0}
-        bankof = {}
-        jobs = []
+        fills, bankof = [], {}
+        jobs, tb_of = [], {}
+        state = {"filled": 0, "used": 0, "tpe": 0, "tact": 0, "tlim": 0}
 
-        def pump():
-            while fills and state["filled"] - state["used"] < NRING:
+        def pump(ring=NRING):
+            while fills and state["filled"] - state["used"] < ring:
                 if not fills[0]():
                     break
                 fills.pop(0)
                 state["filled"] += 1
 
-        def used():
+        def used(ring=NRING):
             state["used"] += 1
-            pump()
+            pump(ring)
 
         def tpump():
-            while state["tpe"] < len(jobs) and state["tpe"] - state["tact"] < 2:
+            while state["tpe"] < min(len(jobs), state["tlim"]) and state["tpe"] - state["tact"] < 2:
                 if not jobs[state["tpe"]][0]():
                     break
                 state["tpe"] += 1
 
         def tjob():
+            state["tlim"] = max(state["tlim"], state["tact"] + 1)
             tpump()
             assert state["tpe"] > state["tact"], "job not ready"
             jobs[state["tact"]][1]()
@@ -108,24 +108,27 @@ def tile_slstmcell_t_kernel(tc, x, h, c, n, m, W_i, b_i, W_f, b_f, W_o, b_o, W_z
             tpump()
             pump()
 
-        def load(dst, q, src, tag):
-            dst[q] = ld.tile([P, QW], BF16, name=tag + "q", tag=tag)
-            nc.sync.dma_start(out=dst[q][:], in_=src[:, q * QW : (q + 1) * QW])
+        def load_m(q):
+            mq[q] = ld.tile([P, QW], BF16, name="mq", tag="m")
+            nc.sync.dma_start(out=mq[q][:], in_=mv[:, q * QW : (q + 1) * QW])
+
+        def load_nc(q):
+            ncq[q] = ld.tile([P, 2 * QW], BF16, name="ncq", tag="nc")
+            nc.sync.dma_start(out=ncq[q][:, 0:QW], in_=nv[:, q * QW : (q + 1) * QW])
+            nc.sync.dma_start(out=ncq[q][:, QW : 2 * QW], in_=cv[:, q * QW : (q + 1) * QW])
 
         def load_xh(q):
             xhq[q] = ld.tile([P, 4 * 512], BF16, name="xhq", tag="xh")
-            for half_, src in enumerate((xv, hv)):
+            for side, src in enumerate((xv, hv)):
                 nc.sync.dma_start(
-                    out=xhq[q][:].rearrange("p (t s d) -> p t s d", t=4, s=2)[:, :, half_, :],
+                    out=xhq[q][:].rearrange("p (t s d) -> p t s d", t=4, s=2)[:, :, side, :],
                     in_=src[:, q * QW : (q + 1) * QW].rearrange("p (t d) -> p t d", t=4),
                 )
 
         def store(g, q, t):
             nc.sync.dma_start(out=ov[g, :, q * QW : (q + 1) * QW], in_=t[:])
 
-        tb_of = {}
-
-        def add_e1(key, ins_fn, out_fn, eng, ready_fn):
+        def add_e1(key, ins_fn, out_fn, eng, ready_fn, after=None):
             def pe():
                 if not ready_fn():
                     return False
@@ -141,47 +144,21 @@ def tile_slstmcell_t_kernel(tc, x, h, c, n, m, W_i, b_i, W_f, b_f, W_o, b_o, W_z
                     nc.scalar.copy(out=out_fn(), in_=src)
                 else:
                     nc.vector.tensor_copy(out=out_fn(), in_=src)
+                if after is not None:
+                    after()
 
             jobs.append((pe, drain))
 
-        def add_e1_w(k, eng):
+        def add_e1_w(k, blk, eng):
             w32 = w_sb[:].bitcast(F32)
-            gw32 = gw[:, 0 : 8 * 512].bitcast(F32).rearrange("p (s c u) -> p s c u", s=8, u=2)
+            gw32 = gw[:].bitcast(F32).rearrange("p (s c u) -> p s c u", s=10, u=2)
             add_e1(
                 ("w", k),
                 lambda: [w32[:, (2 * k + s) * 256 + u : (2 * k + s + 1) * 256 : 2] for s in range(2) for u in range(2)],
-                lambda: gw32[:, 2 * k : 2 * k + 2],
+                lambda: gw32[:, blk : blk + 2],
                 eng,
                 lambda: True,
             )
-
-        def add_e1_pair(j, eng):
-            q, jj = j // 2, j % 2
-
-            def ins():
-                xh32 = xhq[q][:].bitcast(F32)
-                res = []
-                for tt in range(2):
-                    t = 2 * jj + tt
-                    for u in range(2):
-                        res.append(xh32[:, t * 256 + u : (t + 1) * 256 : 2])
-                return res
-
-            def dst():
-                if jj == 0:
-                    gq[q] = grp.tile([P, 4 * 512], BF16, name="g", tag="g", align_bytes=64)
-                g32 = gq[q][:].bitcast(F32).rearrange("p (t c u) -> p t c u", t=4, u=2)
-                return g32[:, 2 * jj : 2 * jj + 2]
-
-            add_e1(("x", j), ins, dst, eng, lambda: q in xhq)
-            if jj == 1 and q + 3 < NQ:
-                pe_, drain_ = jobs.pop()
-
-                def drain_and_load():
-                    drain_()
-                    load_xh(q + 3)
-
-                jobs.append((pe_, drain_and_load))
 
         def add_exit(q, blk, dst, func, bias, scale, tag, bufs, blk2=None):
             key = (tag, q, blk)
@@ -191,21 +168,16 @@ def tile_slstmcell_t_kernel(tc, x, h, c, n, m, W_i, b_i, W_f, b_f, W_o, b_o, W_z
                     return False
                 tbk = ps.tile([P, 512], F32, name="bank_T", tag="T", bufs=2)
                 tb_of[key] = tbk
-                seq = [(blk, True, True)] * DUP
-                if blk2 is None:
-                    seq.append((blk, True, True))
-                else:
-                    seq.append((blk, True, False))
-                    seq.append((blk2, False, True))
-                for bl, st, sp in seq:
+                seq = [blk] if blk2 is None else [blk, blk2]
+                for k, bl in enumerate(seq):
                     nc.tensor.matmul_mx(
                         out=tbk[:],
                         lhsT=wc[:, bl * P : (bl + 1) * P].bitcast(FP8X4),
                         lhsT_scale=wscl[:, bl * P : (bl + 1) * P],
                         rhs=codes[:, q * 512 : (q + 1) * 512].bitcast(FP8X4),
                         rhs_scale=scl[:, q * 512 : (q + 1) * 512],
-                        start=st,
-                        stop=sp,
+                        start=k == 0,
+                        stop=k == len(seq) - 1,
                     )
                 return True
 
@@ -215,19 +187,17 @@ def tile_slstmcell_t_kernel(tc, x, h, c, n, m, W_i, b_i, W_f, b_f, W_o, b_o, W_z
 
             jobs.append((pe, drain))
 
-        quantised_w = {}
-
-        def add_exit_d(q):
+        def add_exit_e(q):
             for r in range(2):
-                add_exit(q, GF + r, dT, ACT.Identity, bd[:, r : r + 1], 1.0, "dT", 2, blk2=GN + r)
+                add_exit(q, GF + r, eT, ACT.Identity, bd[:, r : r + 1], 1.0, "eT", 2, blk2=GN + r)
 
         def add_exit_z(q):
             for r in range(2):
-                add_exit(q, GZ + r, zT, ACT.Tanh, bcol[:, GZ + r : GZ + r + 1], 1.0, "zT", 2)
+                add_exit(q, GZ + r, zT, ACT.Tanh, bcol[:, 4 + r : 5 + r], 1.0, "zT", 2)
 
         def add_exit_o(q):
             for r in range(2):
-                add_exit(q, GO + r, thT, ACT.Tanh, bhalf[:, r : r + 1], 0.5, "thT", 3)
+                add_exit(q, GO + r, thT, ACT.Tanh, bhalf[:, r : r + 1], 0.5, "thT", 4)
 
         def quant(q):
             nc.vector.quantize_mx(
@@ -237,7 +207,8 @@ def tile_slstmcell_t_kernel(tc, x, h, c, n, m, W_i, b_i, W_f, b_f, W_o, b_o, W_z
             )
             quantised[q] = True
             tpump()
-            pump()
+            if q > 0:
+                pump()
 
         def quant_w(s0, nblk):
             nc.vector.quantize_mx(
@@ -248,11 +219,40 @@ def tile_slstmcell_t_kernel(tc, x, h, c, n, m, W_i, b_i, W_f, b_f, W_o, b_o, W_z
             for bl in range(s0, s0 + nblk):
                 quantised_w[bl] = True
             tpump()
-            pump()
 
         def new_bank(key):
             bankof[key] = ps.tile([P, 512], F32, name="bank_B", tag="B", bufs=NRING)
             return bankof[key]
+
+        def add_x(j):
+            q, jj = j // 2, j % 2
+
+            def go():
+                if q not in xhq:
+                    return False
+                bk = new_bank(("X", j))
+                xh32 = xhq[q][:].bitcast(F32)
+                for tt in range(2):
+                    for u in range(2):
+                        t = 2 * jj + tt
+                        nc.tensor.transpose(bk[:, (2 * tt + u) * P : (2 * tt + u + 1) * P], xh32[:, t * 256 + u : (t + 1) * 256 : 2], ident32[:])
+                return True
+
+            fills.append(go)
+
+        def xcopy(j, eng, ring=NRING):
+            q, jj = j // 2, j % 2
+            if jj == 0:
+                gq[q] = grp.tile([P, 4 * 512], BF16, name="g", tag="g", align_bytes=64)
+            dst = gq[q][:].bitcast(F32).rearrange("p (t c u) -> p t c u", t=4, u=2)[:, 2 * jj : 2 * jj + 2]
+            src = bankof[("X", j)][:].rearrange("p (s u c) -> p s c u", s=2, u=2)
+            if eng == "act":
+                nc.scalar.copy(out=dst, in_=src)
+            else:
+                nc.vector.tensor_copy(out=dst, in_=src)
+            used(ring)
+            if jj == 1 and q + 3 < NQ:
+                load_xh(q + 3)
 
         def add_i(j):
             def go():
@@ -274,26 +274,31 @@ def tile_slstmcell_t_kernel(tc, x, h, c, n, m, W_i, b_i, W_f, b_f, W_o, b_o, W_z
 
             fills.append(go)
 
-        def add_back(kind, src, j, plus_m):
+        def back(bk, src, j, plus_m):
             q, jj = j // 2, j % 2
+            if plus_m:
+                nc.tensor.matmul(out=bk[:], lhsT=identb[:], rhs=mq[q][:, jj * PW : (jj + 1) * PW], start=True, stop=False)
+            for tt in range(2):
+                for r in range(2):
+                    o = bk[:, tt * DIM + r * P : tt * DIM + (r + 1) * P]
+                    i = src[(q, r)][:, (2 * jj + tt) * P : (2 * jj + tt + 1) * P]
+                    if plus_m:
+                        nc.tensor.matmul(out=o, lhsT=i, rhs=ident32[:], is_transpose=True, start=False, stop=(tt == 1 and r == 1))
+                    else:
+                        nc.tensor.transpose(o, i, ident32[:])
 
+        def add_back(kind, src, j):
             def go():
-                if (q, 0) not in src or (q, 1) not in src:
+                if (j // 2, 0) not in src or (j // 2, 1) not in src:
                     return False
-                bk = new_bank((kind, j))
-                if plus_m:
-                    nc.tensor.matmul(out=bk[:], lhsT=identb[:], rhs=mq[q][:, jj * PW : (jj + 1) * PW], start=True, stop=False)
-                for tt in range(2):
-                    for r in range(2):
-                        o = bk[:, tt * DIM + r * P : tt * DIM + (r + 1) * P]
-                        i = src[(q, r)][:, (2 * jj + tt) * P : (2 * jj + tt + 1) * P]
-                        if plus_m:
-                            nc.tensor.matmul(out=o, lhsT=i, rhs=ident32[:], is_transpose=True, start=False, stop=(tt == 1 and r == 1))
-                        else:
-                            nc.tensor.transpose(o, i, ident32[:])
+                back(new_bank((kind, j)), src, j, False)
                 return True
 
             fills.append(go)
+
+        def fill_e(j):
+            bankof[("E", j)] = ps.tile([P, 512], F32, name="bank_E", tag="E", bufs=2)
+            back(bankof[("E", j)], eT, j, True)
 
         def half(t, j):
             return t[:, (j % 2) * PW : (j % 2 + 1) * PW]
@@ -307,71 +312,62 @@ def tile_slstmcell_t_kernel(tc, x, h, c, n, m, W_i, b_i, W_f, b_f, W_o, b_o, W_z
             q = j // 2
             if j % 2 == 0:
                 mnq[q] = ost.tile([P, QW], F32, name="mn", tag="mn")
-                e1q[q] = wk.tile([P, QW], F32, name="e1", tag="e1")
-                e2q[q] = wk.tile([P, QW], F32, name="e2", tag="e2")
-            d = bankof[("D", j)]
-            nc.vector.scalar_tensor_tensor(out=half(mnq[q], j), in0=d[:], scalar=0.0, in1=a_t[j][:], op0=ALU.max, op1=ALU.add)
-            nc.scalar.activation(out=half(e1q[q], j), in_=d[:], func=ACT.Exp, scale=-1.0)
-            nc.scalar.activation(out=half(e2q[q], j), in_=d[:], func=ACT.Exp, scale=1.0)
-            used()
+            nc.vector.scalar_tensor_tensor(out=half(mnq[q], j), in0=bankof[("E", j)][:], scalar=0.0, in1=a_t[j][:], op0=ALU.max, op1=ALU.add)
             if j % 2 == 1:
                 store(3, q, mnq[q])
 
-        def v_fn(q):
-            fnq[q] = wk.tile([P, QW], F32, name="fn", tag="fn")
-            nc.vector.scalar_tensor_tensor(out=fnq[q][:], in0=e2q[q][:], scalar=1.0, in1=nq[q][:], op0=ALU.min, op1=ALU.mult)
+        def s_exps(j):
+            q = j // 2
+            if j % 2 == 0:
+                e1q[q] = wk.tile([P, QW], F32, name="e1", tag="e1", bufs=3)
+                e2q[q] = wk.tile([P, QW], F32, name="e2", tag="e2")
+            nc.scalar.activation(out=half(e2q[q], j), in_=bankof[("E", j)][:], func=ACT.Exp, scale=1.0)
+            nc.scalar.activation(out=half(e1q[q], j), in_=bankof[("E", j)][:], func=ACT.Exp, scale=-1.0)
+
+        def v_f(q):
+            fq[q] = wk.tile([P, 2 * QW], F32, name="fnc", tag="fnc", bufs=1)
+            nc.vector.scalar_tensor_tensor(
+                out=fq[q][:].rearrange("p (s d) -> p s d", s=2),
+                in0=e2q[q][:].unsqueeze(1).to_broadcast([P, 2, QW]),
+                scalar=1.0,
+                in1=ncq[q][:].rearrange("p (s d) -> p s d", s=2),
+                op0=ALU.min,
+                op1=ALU.mult,
+            )
 
         def v_nn(q):
-            nnq[q] = ost.tile([P, QW], F32, name="nn", tag="nn", bufs=3 if CN_ON_GPSIMD else 2)
-            nc.vector.scalar_tensor_tensor(out=nnq[q][:], in0=e1q[q][:], scalar=1.0, in1=fnq[q][:], op0=ALU.min, op1=ALU.add)
+            nnq[q] = ost.tile([P, QW], F32, name="nn", tag="nn", bufs=3)
+            nc.vector.scalar_tensor_tensor(out=nnq[q][:], in0=e1q[q][:], scalar=1.0, in1=fq[q][:, 0:QW], op0=ALU.min, op1=ALU.add)
             store(2, q, nnq[q])
+
+        def s_sq(q):
             sqq[q] = ring.tile([P, QW], F32, name="sq", tag="sq")
             nc.scalar.activation(out=sqq[q][:], in_=nnq[q][:], func=ACT.Square, bias=epsc[:], scale=1.0)
-
-        def v_fc(q):
-            nc.vector.scalar_tensor_tensor(out=e2q[q][:], in0=e2q[q][:], scalar=1.0, in1=cq[q][:], op0=ALU.min, op1=ALU.mult)
 
         def v_iz(j):
             e1h = half(e1q[j // 2], j)
             nc.vector.scalar_tensor_tensor(out=e1h, in0=e1h, scalar=1.0, in1=bankof[("Z", j)][:], op0=ALU.min, op1=ALU.mult)
             used()
 
-        def v_cn(q):
-            cnq[q] = ost.tile([P, QW], F32, name="cn", tag="cn", bufs=3 if CN_ON_GPSIMD else 2)
-            if CN_ON_GPSIMD:
-                for t in range(4):
-                    cols = slice(t * DIM, (t + 1) * DIM)
-                    nc.gpsimd.tensor_tensor(out=cnq[q][:, cols], in0=e1q[q][:, cols], in1=e2q[q][:, cols], op=ALU.add)
-            else:
-                nc.vector.tensor_tensor(out=cnq[q][:], in0=e1q[q][:], in1=e2q[q][:], op=ALU.add)
+        def cn(q):
+            cnq[q] = ost.tile([P, QW], F32, name="cn", tag="cn", bufs=2)
+            eng = nc.gpsimd if q in CN_GPSIMD else nc.vector
+            eng.tensor_tensor(out=cnq[q][:], in0=e1q[q][:], in1=fq[q][:, QW : 2 * QW], op=ALU.add)
             store(1, q, cnq[q])
 
-        r2done, p2done = {}, {}
-
-        def g_p2(q):
-            if P2_ON_GPSIMD and q in pq and q in r2done and q not in p2done:
-                p2done[q] = True
-                for t in range(4):
-                    cols = slice(t * DIM, (t + 1) * DIM)
-                    nc.gpsimd.tensor_tensor(out=sqq[q][:, cols], in0=pq[q][:, cols], in1=sqq[q][:, cols], op=ALU.mult)
-
         def v_p(q):
-            pq[q] = ring.tile([P, QW], F32, name="p", tag="p")
+            pq[q] = ring.tile([P, QW], F32, name="p", tag="p", bufs=5)
             nc.vector.scalar_tensor_tensor(out=pq[q][:], in0=nnq[q][:], scalar=EPS, in1=cnq[q][:], op0=ALU.add, op1=ALU.mult)
-            g_p2(q)
 
-        def s_ln(ci):
-            for q in range(CHUNKS[ci][0], CHUNKS[ci][1]):
-                nc.scalar.activation(out=sqq[q][:], in_=sqq[q][:], func=ACT.Ln, scale=2.0)
+        def s_ln(q):
+            nc.scalar.activation(out=sqq[q][:], in_=sqq[q][:], func=ACT.Ln, scale=2.0)
 
         def s_r2(q):
             nc.scalar.activation(out=sqq[q][:], in_=sqq[q][:], func=ACT.Exp, scale=-1.0)
-            r2done[q] = True
-            g_p2(q)
 
-        def v_p2(q):
-            if not P2_ON_GPSIMD:
-                nc.vector.tensor_tensor(out=sqq[q][:], in0=pq[q][:], in1=sqq[q][:], op=ALU.mult)
+        def p2(q):
+            eng = nc.gpsimd if q in P2_GPSIMD else nc.vector
+            eng.tensor_tensor(out=sqq[q][:], in0=pq[q][:], in1=sqq[q][:], op=ALU.mult)
 
         def v_h(j):
             q = j // 2
@@ -382,177 +378,181 @@ def tile_slstmcell_t_kernel(tc, x, h, c, n, m, W_i, b_i, W_f, b_f, W_o, b_o, W_z
             if j % 2 == 1:
                 store(0, q, hhq[q])
 
-        add_e1_w(0, "act")
-        add_e1_w(1, "dve")
-        add_e1_pair(0, "act")
-        add_e1_pair(1, "dve")
-        add_exit_d(0)
-        add_e1_pair(2, "dve")
-        add_e1_pair(3, "dve")
-        add_e1_w(2, "act")
-        add_e1_pair(4, "dve")
-        add_e1_pair(5, "dve")
-        per_it = {}
+        add_e1_w(0, GI, "act")
+        add_e1_w(1, GF, "dve")
+        add_exit_e(0)
+        add_e1_w(2, GZ, "act")
+        plan = {}
         for it in range(NITER):
-            n0 = len(jobs)
+            todo = ""
             if it + 1 < NQ:
-                add_exit_d(it + 1)
+                add_exit_e(it + 1)
+                todo += "ee"
             if it < NQ:
                 add_exit_z(it)
-            for bq in B_AT.get(it + 1, []):
-                add_exit_o(bq)
-            if it + 3 < NQ:
-                add_e1_pair(2 * (it + 3), "act")
-                add_e1_pair(2 * (it + 3) + 1, "act")
+                todo += "zz"
             if it == 0:
-                add_e1_w(3, "act")
-            per_it[it] = len(jobs) - n0
+                add_e1_w(3, GO, "act")
+                todo += "w"
+            for hq in O_AT.get(it, []):
+                add_exit_o(hq)
+                todo += "oo"
+            plan[it] = list(todo)
+        for q in range(3):
+            add_x(2 * q)
+            add_x(2 * q + 1)
         for it in range(NITER):
+            if 1 <= it <= NQ:
+                add_back("Z", zT, 2 * (it - 1))
+                add_back("Z", zT, 2 * (it - 1) + 1)
+            for hq in H_AT.get(it, []) if it < NITER - 1 else [4, 5, 6, 7]:
+                add_back("TH", thT, 2 * hq)
+                add_back("TH", thT, 2 * hq + 1)
             if it < NQ:
                 add_i(2 * it)
                 add_i(2 * it + 1)
-                add_back("D", dT, 2 * it, True)
-                add_back("D", dT, 2 * it + 1, True)
-            if 1 <= it <= NQ:
-                add_back("Z", zT, 2 * (it - 1), False)
-                add_back("Z", zT, 2 * (it - 1) + 1, False)
-            for bq in B_AT.get(it, []):
-                add_back("TH", thT, 2 * bq, False)
-                add_back("TH", thT, 2 * bq + 1, False)
+            if it + 3 < NQ:
+                add_x(2 * (it + 3))
+                add_x(2 * (it + 3) + 1)
 
-        make_identity(nc, ident32[:])
-        nc.vector.memset(brow[:], 0.0)
-        nc.vector.memset(epsc[:], EPS)
-        nc.vector.memset(birow[:], 0.0)
-        nc.vector.memset(ones[:], 1.0)
-        nc.scalar.dma_start(out=brow[0:2, :], in_=b_i.rearrange("(r c) -> r c", r=2))
-        nc.scalar.dma_start(out=brow[2:4, :], in_=b_f.rearrange("(r c) -> r c", r=2))
-        nc.scalar.dma_start(out=birow[0:1, :], in_=b_i.rearrange("(r c) -> r c", r=1))
-        nc.scalar.dma_start(out=brow[4:6, :], in_=b_z.rearrange("(r c) -> r c", r=2))
-        nc.scalar.dma_start(out=brow[6:8, :], in_=b_o.rearrange("(r c) -> r c", r=2))
-
-        def load_w(s0, wg):
+        def load_w(k, wg):
             nc.sync.dma_start(
-                out=w_sb[:, s0 * 512 : (s0 + 2) * 512].rearrange("p (r k) -> p r k", r=2),
+                out=w_sb[:, 2 * k * 512 : (2 * k + 2) * 512].rearrange("p (r k) -> p r k", r=2),
                 in_=wg.rearrange("(r p) k -> p r k", p=P),
             )
 
-        load_w(GI, W_i)
-        load_w(GF, W_f)
+        nc.vector.memset(epsc[:], EPS)
+        nc.scalar.activation(out=dummy[:], in_=epsc[:], func=ACT.Exp)
+        make_identity(nc, ident32[:])
+        load_w(0, W_i)
+        load_w(1, W_f)
         load_xh(0)
-        load(mq, 0, mv, "m")
+        nc.vector.memset(brow[:], 0.0)
+        nc.vector.memset(birow[:], 0.0)
+        nc.vector.memset(ones[:], 1.0)
+        nc.sync.dma_start(out=brow[0:2, :], in_=b_i.rearrange("(r c) -> r c", r=2))
+        nc.sync.dma_start(out=brow[2:4, :], in_=b_f.rearrange("(r c) -> r c", r=2))
+        nc.sync.dma_start(out=brow[4:6, :], in_=b_z.rearrange("(r c) -> r c", r=2))
+        nc.sync.dma_start(out=brow[6:8, :], in_=b_o.rearrange("(r c) -> r c", r=2))
+        nc.sync.dma_start(out=birow[0:1, :], in_=b_i.rearrange("(r c) -> r c", r=1))
+        load_m(0)
         load_xh(1)
-        load_w(GZ, W_z)
+        load_w(2, W_z)
+        load_nc(0)
         load_xh(2)
-        load(cq, 0, cv, "c")
-        load(nq, 0, nv, "n")
-        load(mq, 1, mv, "m")
-        load_w(GO, W_o)
+        load_m(1)
+        load_w(3, W_o)
 
         nc.vector.tensor_copy(out=identb[:], in_=ident32[:])
+        state["tlim"] = 2
+        tpump()
+        pump(2)
         tjob()
         tjob()
         nc.vector.tensor_scalar(out=gw[:, GN * 512 : (GN + 2) * 512], in0=gw[:, GI * 512 : (GI + 2) * 512], scalar1=-1.0, scalar2=None, op0=ALU.mult)
-        quant_w(GI, 4)
-        tjob()
-        tjob()
-        tb = ps.tile([P, 512], F32, name="bank_B", tag="B", bufs=NRING)
+        quant_w(GF, 4)
+        tb = ps.tile([P, 512], F32, name="bank_E", tag="E", bufs=2)
         tbb = tb[:].bitcast(BF16)
         nc.tensor.transpose(tbb[:, 0:P], brow[:], identb[:])
-        nc.vector.tensor_copy(out=bcol[:], in_=tbb[:, 0:8])
         nc.tensor.matmul(out=tb[:, DIM : 2 * DIM], lhsT=ones[:], rhs=birow[:], start=True, stop=True)
+        xcopy(0, "act", 2)
+        xcopy(1, "dve", 2)
+        state["tlim"] = 4
+        quant(0)
+        nc.vector.tensor_copy(out=bcol[:], in_=tbb[:, 0:10])
+        pump()
+        nc.vector.tensor_tensor(out=bd[:], in0=bcol[:, 2:4], in1=bcol[:, 0:2], op=ALU.subtract)
+        tjob()
+        tjob()
+        nc.vector.tensor_scalar(out=bhalf[:], in0=bcol[:, 6:8], scalar1=0.5, scalar2=None, op0=ALU.mult)
         for r in range(2):
             nc.vector.tensor_copy(out=bib[:, r * DIM : (r + 1) * DIM], in_=tb[:, DIM : 2 * DIM])
-        nc.vector.tensor_scalar(out=bhalf[:], in0=bcol[:, GO : GO + 2], scalar1=0.5, scalar2=None, op0=ALU.mult)
-        nc.vector.tensor_tensor(out=bd[:], in0=bcol[:, GF : GF + 2], in1=bcol[:, GI : GI + 2], op=ALU.subtract)
-        state["filled"] += 1
-        state["used"] += 1
-
-        quant_w(GN, 2)
-        quant(0)
+        fill_e(0)
+        fill_e(1)
+        quant_w(GI, 2)
+        xcopy(2, "dve")
+        xcopy(3, "dve")
+        quant(1)
         tjob()
-        tjob()
-        pump()
+        xcopy(4, "dve")
+        xcopy(5, "dve")
+        quant_w(GZ, 2)
 
-        def startup(it, pos):
-            if it == 0 and pos == 0:
-                tjob()
-                tjob()
-                tjob()
-                tjob()
-                tjob()
-            if it == 0 and pos == 1:
-                quant(1)
-                quant_w(GZ, 2)
-                quant(2)
-            if it == 1 and pos == 3:
-                quant_w(GO, 2)
+        s_exps(0)
+        s_exps(1)
 
-        for it in range(NITER):
+        for it in range(NITER - 1):
             qa = it if it < NQ else None
             qk = it - 1 if 1 <= it <= NQ else None
-            bs = B_AT.get(it, [])
-            b0 = bs[0] if bs else None
-            todo = per_it[it]
+            qp = it - 2 if 2 <= it <= NQ + 1 else None
             if it + 2 < NQ:
-                load(mq, it + 2, mv, "m")
+                load_m(it + 2)
             if it + 1 < NQ:
-                load(cq, it + 1, cv, "c")
-                load(nq, it + 1, nv, "n")
+                load_nc(it + 1)
+            todo = plan[it]
 
-            def act_jobs(k):
-                for z_ in range(k):
+            def act_jobs(kinds, ahead=0):
+                k = 0
+                while k < len(todo) and todo[k] in kinds:
+                    k += 1
+                state["tlim"] = state["tact"] + k + ahead
+                for i in range(k):
+                    todo.pop(0)
                     tjob()
 
-            first = min(4, todo) if it > 0 else 0
-            act_jobs(first)
-            todo -= first
+            if qk is not None:
+                v_f(qk)
+            act_jobs("e")
+            if qk == NQ - 1:
+                v_nn(qk)
+                s_sq(qk)
+                s_ln(qk)
+                for rq in range(4, NQ):
+                    s_r2(rq)
+            if qp is not None:
+                v_p(qp)
+            act_jobs("z")
+            act_jobs("w")
+            if qk is not None and qk < NQ - 1:
+                v_nn(qk)
+            if 2 <= it + 2 < NQ:
+                quant(it + 2)
+            if qk is not None and qk < NQ - 1:
+                s_sq(qk)
+            if qk is not None:
+                v_iz(2 * qk)
+                v_iz(2 * qk + 1)
+                cn(qk)
+            act_jobs("o")
+            for pq_ in P2_AT.get(it, []):
+                p2(pq_)
+            for hq in H_AT.get(it, []):
+                v_h(2 * hq)
+                v_h(2 * hq + 1)
+            for rq in R2_AT.get(it, []) if it not in LN_AT else []:
+                s_r2(rq)
             if qa is not None:
                 v_a(2 * qa)
                 v_a(2 * qa + 1)
-            if CN_ON_GPSIMD and 2 <= it <= NQ + 1:
-                v_p(it - 2)
-            if qk is not None:
-                v_fn(qk)
-            if qa is not None:
                 v_mn(2 * qa)
-            if qk is not None:
-                v_nn(qk)
-            startup(it, 0)
-            if qk is not None:
-                v_fc(qk)
-            if qa is not None:
                 v_mn(2 * qa + 1)
-            startup(it, 1)
-            startup(it, 2)
-            if qk is not None:
-                v_iz(2 * qk)
-            if b0 is not None:
-                v_p2(b0)
-            if qk is not None:
-                v_iz(2 * qk + 1)
-            if b0 is not None:
-                v_h(2 * b0)
-            if qk is not None:
-                v_cn(qk)
-            if b0 is not None:
-                v_h(2 * b0 + 1)
-            if qk is not None and not CN_ON_GPSIMD:
-                v_p(qk)
-            startup(it, 3)
-            act_jobs(todo)
-            fresh = range(CHUNKS[ln_at[it]][0], CHUNKS[ln_at[it]][1]) if it in ln_at else []
-            for bq in B_AT.get(it + 1, []):
-                if bq not in fresh:
-                    s_r2(bq)
-            if it in ln_at:
-                s_ln(ln_at[it])
-            for bq in B_AT.get(it + 1, []):
-                if bq in fresh:
-                    s_r2(bq)
-            for bq in bs[1:]:
-                v_p2(bq)
-                v_h(2 * bq)
-                v_h(2 * bq + 1)
-            if 3 <= it + 2 < NQ:
-                quant(it + 2)
+            if it + 1 < NQ:
+                fill_e(2 * (it + 1))
+                fill_e(2 * (it + 1) + 1)
+            if it + 3 < NQ:
+                for j in (2 * (it + 3), 2 * (it + 3) + 1):
+                    xcopy(j, "act" if j in X_SCALAR else "dve")
+            if it + 1 < NQ:
+                s_exps(2 * (it + 1))
+                s_exps(2 * (it + 1) + 1)
+            if it == 0:
+                quant_w(GO, 2)
+            for lq in LN_AT.get(it, []):
+                s_ln(lq)
+            for rq in R2_AT.get(it, []) if it in LN_AT else []:
+                s_r2(rq)
+        v_p(NQ - 1)
+        for hq in range(4, NQ):
+            p2(hq)
+            v_h(2 * hq)
+            v_h(2 * hq + 1)

@@ -21,15 +21,10 @@ QW = 4 * DIM
 EPS = 1e-6
 FLOPS = 2 * B * 2 * DIM * 4 * DIM
 
-LN_AT = {4: [0, 1, 2, 3], 7: [4, 5, 6]}
-R2_AT = {4: [0], 5: [1, 2], 6: [3]}
-O_AT = {3: [0], 4: [1], 5: [2], 6: [3, 4], 7: [5, 6, 7]}
-P2_AT = {5: [0], 6: [1, 2], 7: [3]}
-H_AT = {6: [0], 7: [1, 2], 8: [3]}
-P2_GPSIMD = [0, 1, 2, 3]
+O_AT = {3: [0], 4: [1], 5: [2], 6: [3]}
+P2_GPSIMD = [2, 4, 6]
 CN_GPSIMD = [0, 1, 2, 3, 4, 5, 6]
 X_SCALAR = [6, 7, 8, 9, 10, 11, 12, 13, 14, 15]
-NITER = NQ + 2
 GI, GF, GN, GZ, GO = 0, 2, 4, 6, 8
 NRING = 4
 
@@ -52,8 +47,7 @@ def tile_slstmcell_t_kernel(tc, x, h, c, n, m, W_i, b_i, W_f, b_f, W_o, b_o, W_z
         gt = ctx.enter_context(tc.tile_pool(name="gt", bufs=2))
         wk = ctx.enter_context(tc.tile_pool(name="wk", bufs=2))
         ost = ctx.enter_context(tc.tile_pool(name="ost", bufs=2))
-        wst = ctx.enter_context(tc.tile_pool(name="wst", bufs=1))
-        ring = ctx.enter_context(tc.tile_pool(name="ring", bufs=7))
+        ring = ctx.enter_context(tc.tile_pool(name="ring", bufs=8))
 
         ident32 = const.tile([P, P], F32, name="ident32")
         identb = const.tile([P, P], BF16, name="identb")
@@ -63,19 +57,17 @@ def tile_slstmcell_t_kernel(tc, x, h, c, n, m, W_i, b_i, W_f, b_f, W_o, b_o, W_z
         bd = const.tile([P, 2], F32, name="bd")
         epsc = const.tile([P, 1], F32, name="epsc")
         bib = const.tile([P, PW], BF16, name="bib")
-        birow = const.tile([P, DIM], BF16, name="birow")
-        ones = const.tile([P, P], BF16, name="ones")
         wc = const.tile([P, 10 * P], U32, name="wc", align_bytes=64)
         wscl = const.tile([P, 10 * P], U8, name="wscl", align_bytes=64)
         codes = const.tile([P, B], U32, name="codes", align_bytes=64)
         scl = const.tile([P, B], U8, name="scl", align_bytes=64)
         dummy = const.tile([P, 1], F32, name="dummy")
-        w_sb = wst.tile([P, 8 * 512], BF16, name="w_sb")
-        gw = wst.tile([P, 10 * 512], BF16, name="gw", align_bytes=64)
+        w_sb = [ring.tile([P, 4 * 512], BF16, name="w_sb", tag="cn", align_bytes=64) for half_ in range(2)]
+        gw = [ring.tile([P, 4 * 512], BF16, name="gw", tag="cn", align_bytes=64) for half_ in range(3)]
 
         xhq, mq, ncq, gq = {}, {}, {}, {}
         eT, zT, thT = {}, {}, {}
-        e1q, e2q, fq, nnq, cnq, mnq, hhq, pq, sqq, a_t = {}, {}, {}, {}, {}, {}, {}, {}, {}, {}
+        e1q, e2q, fq, nnq, cnq, mnq, sqq, a_t = {}, {}, {}, {}, {}, {}, {}, {}
         quantised, quantised_w = {}, {}
 
         fills, bankof = [], {}
@@ -99,14 +91,14 @@ def tile_slstmcell_t_kernel(tc, x, h, c, n, m, W_i, b_i, W_f, b_f, W_o, b_o, W_z
                     break
                 state["tpe"] += 1
 
-        def tjob():
+        def tjob(ring=NRING):
             state["tlim"] = max(state["tlim"], state["tact"] + 1)
             tpump()
             assert state["tpe"] > state["tact"], "job not ready"
             jobs[state["tact"]][1]()
             state["tact"] += 1
             tpump()
-            pump()
+            pump(ring)
 
         def load_m(q):
             mq[q] = ld.tile([P, QW], BF16, name="mq", tag="m")
@@ -149,13 +141,17 @@ def tile_slstmcell_t_kernel(tc, x, h, c, n, m, W_i, b_i, W_f, b_f, W_o, b_o, W_z
 
             jobs.append((pe, drain))
 
+        def gw_of(blk, nblk):
+            t, b0 = {GI: (1, GI), GF: (0, GF), GN: (0, GF), GZ: (2, GZ), GO: (2, GZ)}[blk]
+            return gw[t][:, (blk - b0) * 512 : (blk - b0 + nblk) * 512]
+
         def add_e1_w(k, blk, eng):
-            w32 = w_sb[:].bitcast(F32)
-            gw32 = gw[:].bitcast(F32).rearrange("p (s c u) -> p s c u", s=10, u=2)
+            w32 = w_sb[k // 2][:].bitcast(F32)
+            gw32 = gw_of(blk, 2).bitcast(F32).rearrange("p (s c u) -> p s c u", s=2, u=2)
             add_e1(
                 ("w", k),
-                lambda: [w32[:, (2 * k + s) * 256 + u : (2 * k + s + 1) * 256 : 2] for s in range(2) for u in range(2)],
-                lambda: gw32[:, blk : blk + 2],
+                lambda: [w32[:, (2 * (k % 2) + s) * 256 + u : (2 * (k % 2) + s + 1) * 256 : 2] for s in range(2) for u in range(2)],
+                lambda: gw32,
                 eng,
                 lambda: True,
             )
@@ -214,7 +210,7 @@ def tile_slstmcell_t_kernel(tc, x, h, c, n, m, W_i, b_i, W_f, b_f, W_o, b_o, W_z
             nc.vector.quantize_mx(
                 out=wc[:, s0 * P : (s0 + nblk) * P].bitcast(FP8X4),
                 scales=wscl[:, s0 * P : (s0 + nblk) * P],
-                in_=gw[:, s0 * 512 : (s0 + nblk) * 512],
+                in_=gw_of(s0, nblk),
             )
             for bl in range(s0, s0 + nblk):
                 quantised_w[bl] = True
@@ -336,7 +332,7 @@ def tile_slstmcell_t_kernel(tc, x, h, c, n, m, W_i, b_i, W_f, b_f, W_o, b_o, W_z
             )
 
         def v_nn(q):
-            nnq[q] = ost.tile([P, QW], F32, name="nn", tag="nn", bufs=3)
+            nnq[q] = ring.tile([P, QW], F32, name="nn", tag="nn")
             nc.vector.scalar_tensor_tensor(out=nnq[q][:], in0=e1q[q][:], scalar=1.0, in1=fq[q][:, 0:QW], op0=ALU.min, op1=ALU.add)
             store(2, q, nnq[q])
 
@@ -349,15 +345,17 @@ def tile_slstmcell_t_kernel(tc, x, h, c, n, m, W_i, b_i, W_f, b_f, W_o, b_o, W_z
             nc.vector.scalar_tensor_tensor(out=e1h, in0=e1h, scalar=1.0, in1=bankof[("Z", j)][:], op0=ALU.min, op1=ALU.mult)
             used()
 
-        def cn(q):
-            cnq[q] = ost.tile([P, QW], F32, name="cn", tag="cn", bufs=2)
+        def cn(j):
+            q = j // 2
+            if j % 2 == 0:
+                cnq[q] = ring.tile([P, QW], F32, name="cn", tag="cn", align_bytes=64)
             eng = nc.gpsimd if q in CN_GPSIMD else nc.vector
-            eng.tensor_tensor(out=cnq[q][:], in0=e1q[q][:], in1=fq[q][:, QW : 2 * QW], op=ALU.add)
-            store(1, q, cnq[q])
+            eng.tensor_tensor(out=half(cnq[q], j), in0=half(e1q[q], j), in1=half(fq[q][:, QW : 2 * QW], j), op=ALU.add)
+            if j % 2 == 1:
+                store(1, q, cnq[q])
 
         def v_p(q):
-            pq[q] = ring.tile([P, QW], F32, name="p", tag="p", bufs=5)
-            nc.vector.scalar_tensor_tensor(out=pq[q][:], in0=nnq[q][:], scalar=EPS, in1=cnq[q][:], op0=ALU.add, op1=ALU.mult)
+            nc.vector.scalar_tensor_tensor(out=nnq[q][:], in0=nnq[q][:], scalar=EPS, in1=cnq[q][:], op0=ALU.add, op1=ALU.mult)
 
         def s_ln(q):
             nc.scalar.activation(out=sqq[q][:], in_=sqq[q][:], func=ACT.Ln, scale=2.0)
@@ -367,23 +365,22 @@ def tile_slstmcell_t_kernel(tc, x, h, c, n, m, W_i, b_i, W_f, b_f, W_o, b_o, W_z
 
         def p2(q):
             eng = nc.gpsimd if q in P2_GPSIMD else nc.vector
-            eng.tensor_tensor(out=sqq[q][:], in0=pq[q][:], in1=sqq[q][:], op=ALU.mult)
+            eng.tensor_tensor(out=sqq[q][:], in0=nnq[q][:], in1=sqq[q][:], op=ALU.mult)
 
         def v_h(j):
             q = j // 2
-            if j % 2 == 0:
-                hhq[q] = ost.tile([P, QW], F32, name="hh", tag="hh")
-            nc.vector.scalar_tensor_tensor(out=half(hhq[q], j), in0=bankof[("TH", j)][:], scalar=1.0, in1=half(sqq[q], j), op0=ALU.add, op1=ALU.mult)
+            nc.vector.scalar_tensor_tensor(out=half(sqq[q], j), in0=bankof[("TH", j)][:], scalar=1.0, in1=half(sqq[q], j), op0=ALU.add, op1=ALU.mult)
             used()
             if j % 2 == 1:
-                store(0, q, hhq[q])
+                store(0, q, sqq[q])
 
         add_e1_w(0, GI, "act")
         add_e1_w(1, GF, "dve")
-        add_exit_e(0)
         add_e1_w(2, GZ, "act")
+        add_e1_w(3, GO, "act")
+        add_exit_e(0)
         plan = {}
-        for it in range(NITER):
+        for it in range(NQ + 1):
             todo = ""
             if it + 1 < NQ:
                 add_exit_e(it + 1)
@@ -391,9 +388,6 @@ def tile_slstmcell_t_kernel(tc, x, h, c, n, m, W_i, b_i, W_f, b_f, W_o, b_o, W_z
             if it < NQ:
                 add_exit_z(it)
                 todo += "zz"
-            if it == 0:
-                add_e1_w(3, GO, "act")
-                todo += "w"
             for hq in O_AT.get(it, []):
                 add_exit_o(hq)
                 todo += "oo"
@@ -401,90 +395,90 @@ def tile_slstmcell_t_kernel(tc, x, h, c, n, m, W_i, b_i, W_f, b_f, W_o, b_o, W_z
         for q in range(3):
             add_x(2 * q)
             add_x(2 * q + 1)
-        for it in range(NITER):
+        for q in range(4, NQ):
+            add_exit_o(q)
+        for it in range(NQ + 1):
             if 1 <= it <= NQ:
                 add_back("Z", zT, 2 * (it - 1))
                 add_back("Z", zT, 2 * (it - 1) + 1)
-            for hq in H_AT.get(it, []) if it < NITER - 1 else [4, 5, 6, 7]:
-                add_back("TH", thT, 2 * hq)
-                add_back("TH", thT, 2 * hq + 1)
             if it < NQ:
                 add_i(2 * it)
                 add_i(2 * it + 1)
             if it + 3 < NQ:
                 add_x(2 * (it + 3))
                 add_x(2 * (it + 3) + 1)
+        for q in range(NQ):
+            add_back("TH", thT, 2 * q)
+            add_back("TH", thT, 2 * q + 1)
 
         def load_w(k, wg):
             nc.sync.dma_start(
-                out=w_sb[:, 2 * k * 512 : (2 * k + 2) * 512].rearrange("p (r k) -> p r k", r=2),
+                out=w_sb[k // 2][:, 2 * (k % 2) * 512 : (2 * (k % 2) + 2) * 512].rearrange("p (r k) -> p r k", r=2),
                 in_=wg.rearrange("(r p) k -> p r k", p=P),
             )
 
+        nc.vector.memset(brow[:], 0.0)
         nc.vector.memset(epsc[:], EPS)
-        nc.scalar.activation(out=dummy[:], in_=epsc[:], func=ACT.Exp)
         make_identity(nc, ident32[:])
         load_w(0, W_i)
         load_w(1, W_f)
         load_xh(0)
-        nc.vector.memset(brow[:], 0.0)
-        nc.vector.memset(birow[:], 0.0)
-        nc.vector.memset(ones[:], 1.0)
-        nc.sync.dma_start(out=brow[0:2, :], in_=b_i.rearrange("(r c) -> r c", r=2))
-        nc.sync.dma_start(out=brow[2:4, :], in_=b_f.rearrange("(r c) -> r c", r=2))
-        nc.sync.dma_start(out=brow[4:6, :], in_=b_z.rearrange("(r c) -> r c", r=2))
-        nc.sync.dma_start(out=brow[6:8, :], in_=b_o.rearrange("(r c) -> r c", r=2))
-        nc.sync.dma_start(out=birow[0:1, :], in_=b_i.rearrange("(r c) -> r c", r=1))
+        for g, bg in enumerate((b_i, b_f, b_z, b_o)):
+            nc.scalar.dma_start(out=brow[2 * g : 2 * g + 2, :], in_=bg.rearrange("(r c) -> r c", r=2))
+        nc.scalar.activation(out=dummy[:], in_=epsc[:], func=ACT.Exp)
         load_m(0)
-        load_xh(1)
         load_w(2, W_z)
+        load_w(3, W_o)
+        load_xh(1)
         load_nc(0)
         load_xh(2)
         load_m(1)
-        load_w(3, W_o)
 
         nc.vector.tensor_copy(out=identb[:], in_=ident32[:])
         state["tlim"] = 2
         tpump()
-        pump(2)
-        tjob()
-        tjob()
-        nc.vector.tensor_scalar(out=gw[:, GN * 512 : (GN + 2) * 512], in0=gw[:, GI * 512 : (GI + 2) * 512], scalar1=-1.0, scalar2=None, op0=ALU.mult)
-        quant_w(GF, 4)
         tb = ps.tile([P, 512], F32, name="bank_E", tag="E", bufs=2)
         tbb = tb[:].bitcast(BF16)
         nc.tensor.transpose(tbb[:, 0:P], brow[:], identb[:])
-        nc.tensor.matmul(out=tb[:, DIM : 2 * DIM], lhsT=ones[:], rhs=birow[:], start=True, stop=True)
-        xcopy(0, "act", 2)
-        xcopy(1, "dve", 2)
-        state["tlim"] = 4
-        quant(0)
+        for r in range(2):
+            nc.tensor.matmul(out=tb[:, DIM + r * P : DIM + (r + 1) * P], lhsT=identb[:, r : r + 1].to_broadcast([P, P]), rhs=brow[:], start=True, stop=True)
         nc.vector.tensor_copy(out=bcol[:], in_=tbb[:, 0:10])
-        pump()
         nc.vector.tensor_tensor(out=bd[:], in0=bcol[:, 2:4], in1=bcol[:, 0:2], op=ALU.subtract)
-        tjob()
-        tjob()
         nc.vector.tensor_scalar(out=bhalf[:], in0=bcol[:, 6:8], scalar1=0.5, scalar2=None, op0=ALU.mult)
         for r in range(2):
             nc.vector.tensor_copy(out=bib[:, r * DIM : (r + 1) * DIM], in_=tb[:, DIM : 2 * DIM])
+        pump(2)
+        tjob(0)
+        tjob(0)
+        nc.vector.tensor_scalar(out=gw_of(GN, 2), in0=gw_of(GI, 2), scalar1=-1.0, scalar2=None, op0=ALU.mult)
+        quant_w(GF, 4)
+        xcopy(0, "act", 0)
+        xcopy(1, "dve", 0)
+        state["tlim"] = 6
+        tpump()
+        tjob(0)
+        tjob(0)
+        quant(0)
+        quant_w(GI, 2)
+        quant_w(GZ, 4)
+        pump(2)
+        tjob(2)
+        tjob(2)
         fill_e(0)
         fill_e(1)
-        quant_w(GI, 2)
-        xcopy(2, "dve")
-        xcopy(3, "dve")
-        quant(1)
-        tjob()
-        xcopy(4, "dve")
-        xcopy(5, "dve")
-        quant_w(GZ, 2)
-
+        pump()
         s_exps(0)
         s_exps(1)
+        xcopy(2, "dve", 0)
+        xcopy(3, "dve", 0)
+        state["tlim"] = 8
+        quant(1)
+        xcopy(4, "dve")
+        xcopy(5, "dve")
 
-        for it in range(NITER - 1):
+        for it in range(NQ + 1):
             qa = it if it < NQ else None
             qk = it - 1 if 1 <= it <= NQ else None
-            qp = it - 2 if 2 <= it <= NQ + 1 else None
             if it + 2 < NQ:
                 load_m(it + 2)
             if it + 1 < NQ:
@@ -507,30 +501,25 @@ def tile_slstmcell_t_kernel(tc, x, h, c, n, m, W_i, b_i, W_f, b_f, W_o, b_o, W_z
                 v_nn(qk)
                 s_sq(qk)
                 s_ln(qk)
-                for rq in range(4, NQ):
-                    s_r2(rq)
-            if qp is not None:
-                v_p(qp)
+
             act_jobs("z")
-            act_jobs("w")
+            if it == NQ - 1:
+                for q in range(NQ - 2):
+                    s_ln(q)
             if qk is not None and qk < NQ - 1:
                 v_nn(qk)
             if 2 <= it + 2 < NQ:
                 quant(it + 2)
             if qk is not None and qk < NQ - 1:
                 s_sq(qk)
+            if it == NQ - 1:
+                s_ln(NQ - 2)
             if qk is not None:
                 v_iz(2 * qk)
                 v_iz(2 * qk + 1)
-                cn(qk)
+                cn(2 * qk)
+                cn(2 * qk + 1)
             act_jobs("o")
-            for pq_ in P2_AT.get(it, []):
-                p2(pq_)
-            for hq in H_AT.get(it, []):
-                v_h(2 * hq)
-                v_h(2 * hq + 1)
-            for rq in R2_AT.get(it, []) if it not in LN_AT else []:
-                s_r2(rq)
             if qa is not None:
                 v_a(2 * qa)
                 v_a(2 * qa + 1)
@@ -545,14 +534,29 @@ def tile_slstmcell_t_kernel(tc, x, h, c, n, m, W_i, b_i, W_f, b_f, W_o, b_o, W_z
             if it + 1 < NQ:
                 s_exps(2 * (it + 1))
                 s_exps(2 * (it + 1) + 1)
-            if it == 0:
-                quant_w(GO, 2)
-            for lq in LN_AT.get(it, []):
-                s_ln(lq)
-            for rq in R2_AT.get(it, []) if it in LN_AT else []:
-                s_r2(rq)
-        v_p(NQ - 1)
-        for hq in range(4, NQ):
-            p2(hq)
-            v_h(2 * hq)
-            v_h(2 * hq + 1)
+        for q in range(NQ):
+            v_p(q)
+
+        def exit_o(q):
+            state["tlim"] = state["tact"] + 2
+            tjob()
+            tjob()
+
+        s_r2(0)
+        s_r2(1)
+        p2(0)
+        p2(1)
+        for q in range(0, NQ, 2):
+            if q + 2 < NQ:
+                s_r2(q + 2)
+                s_r2(q + 3)
+                p2(q + 2)
+                exit_o(4 + q // 2)
+            v_h(2 * q)
+            v_h(2 * q + 1)
+            v_h(2 * q + 2)
+            v_h(2 * q + 3)
+            if q == 4:
+                exit_o(7)
+            if q + 2 < NQ:
+                p2(q + 3)

@@ -371,7 +371,9 @@ def tile_slstmcell_t_kernel(tc, x, h, c, n, m, W_i, b_i, W_f, b_f, W_o, b_o, W_z
             q = j // 2
             nc.vector.scalar_tensor_tensor(out=half(sqq[q], j), in0=bankof[("TH", j)][:], scalar=1.0, in1=half(sqq[q], j), op0=ALU.add, op1=ALU.mult)
             used()
-            if j % 2 == 1:
+            if q == NQ - 1:
+                nc.sync.dma_start(out=ov[0, :, j * PW : (j + 1) * PW], in_=half(sqq[q], j))
+            elif j % 2 == 1:
                 store(0, q, sqq[q])
 
         add_e1_w(0, GI, "act")
@@ -435,7 +437,7 @@ def tile_slstmcell_t_kernel(tc, x, h, c, n, m, W_i, b_i, W_f, b_f, W_o, b_o, W_z
         load_m(1)
 
         nc.vector.tensor_copy(out=identb[:], in_=ident32[:])
-        state["tlim"] = 2
+        state["tlim"] = 1
         tpump()
         tb = ps.tile([P, 512], F32, name="bank_E", tag="E", bufs=2)
         tbb = tb[:].bitcast(BF16)
@@ -447,6 +449,8 @@ def tile_slstmcell_t_kernel(tc, x, h, c, n, m, W_i, b_i, W_f, b_f, W_o, b_o, W_z
         nc.vector.tensor_scalar(out=bhalf[:], in0=bcol[:, 6:8], scalar1=0.5, scalar2=None, op0=ALU.mult)
         for r in range(2):
             nc.vector.tensor_copy(out=bib[:, r * DIM : (r + 1) * DIM], in_=tb[:, DIM : 2 * DIM])
+        state["tlim"] = 2
+        tpump()
         pump(2)
         tjob(0)
         tjob(0)
@@ -538,10 +542,11 @@ def tile_slstmcell_t_kernel(tc, x, h, c, n, m, W_i, b_i, W_f, b_f, W_o, b_o, W_z
             v_p(q)
 
         def exit_o(q):
-            state["tlim"] = state["tact"] + 2
             tjob()
             tjob()
 
+        state["tlim"] = len(jobs)
+        tpump()
         s_r2(0)
         s_r2(1)
         p2(0)

@@ -24,7 +24,7 @@ FLOPS = 2 * B * 2 * DIM * 4 * DIM
 O_AT = {3: [0], 4: [1], 5: [2], 6: [3]}
 P2_GPSIMD = [2, 4, 6]
 CN_GPSIMD = [0, 1, 2, 3, 4, 5, 6]
-X_SCALAR = [6, 7, 8, 9, 10, 11, 12, 13, 14, 15]
+X_SCALAR = [6, 7, 8, 9, 10, 11, 12, 13]
 GI, GF, GN, GZ, GO = 0, 2, 4, 6, 8
 NRING = 4
 

from contextlib import ExitStack

import concourse.mybir as mybir
from concourse.masks import make_identity

F32 = mybir.dt.float32
BF16 = mybir.dt.bfloat16
U32 = mybir.dt.uint32
U8 = mybir.dt.uint8
FP8X4 = mybir.dt.float8_e4m3fn_x4
ACT = mybir.ActivationFunctionType
ALU = mybir.AluOpType

P = 128
B = 4096
DIM = 256
NT = B // P
NQ = NT // 4
PW = 2 * DIM
QW = 4 * DIM
EPS = 1e-6
FLOPS = 2 * B * 2 * DIM * 4 * DIM

O_AT = {3: [0], 4: [1], 5: [2], 6: [3]}
P2_GPSIMD = [2, 4, 6]
CN_GPSIMD = [0, 1, 2, 3, 4, 5, 6]
X_SCALAR = [6, 7, 8, 9, 10, 11, 12, 13]
GI, GF, GN, GZ, GO = 0, 2, 4, 6, 8
NRING = 4


def tile_slstmcell_t_kernel(tc, x, h, c, n, m, W_i, b_i, W_f, b_f, W_o, b_o, W_z, b_z, out):
    nc = tc.nc
    xv = x.rearrange("(p t) d -> p (t d)", t=NT)
    hv = h.rearrange("(p t) d -> p (t d)", t=NT)
    cv = c.rearrange("(p t) d -> p (t d)", t=NT)
    nv = n.rearrange("(p t) d -> p (t d)", t=NT)
    mv = m.rearrange("(p t) d -> p (t d)", t=NT)
    ov = out.rearrange("g (p t) d -> g p (t d)", t=NT)

    with ExitStack() as ctx:
        ctx.enter_context(tc.manual_schedule())
        const = ctx.enter_context(tc.tile_pool(name="const", bufs=1))
        ps = ctx.enter_context(tc.psum_pool(name="ps", bufs=1))
        ld = ctx.enter_context(tc.tile_pool(name="ld", bufs=3))
        grp = ctx.enter_context(tc.tile_pool(name="grp", bufs=2))
        gt = ctx.enter_context(tc.tile_pool(name="gt", bufs=2))
        wk = ctx.enter_context(tc.tile_pool(name="wk", bufs=2))
        ost = ctx.enter_context(tc.tile_pool(name="ost", bufs=2))
        ring = ctx.enter_context(tc.tile_pool(name="ring", bufs=8))

        ident32 = const.tile([P, P], F32, name="ident32")
        identb = const.tile([P, P], BF16, name="identb")
        brow = const.tile([P, P], BF16, name="brow")
        bcol = const.tile([P, 10], F32, name="bcol")
        bhalf = const.tile([P, 2], F32, name="bhalf")
        bd = const.tile([P, 2], F32, name="bd")
        epsc = const.tile([P, 1], F32, name="epsc")
        bib = const.tile([P, PW], BF16, name="bib")
        wc = const.tile([P, 10 * P], U32, name="wc", align_bytes=64)
        wscl = const.tile([P, 10 * P], U8, name="wscl", align_bytes=64)
        codes = const.tile([P, B], U32, name="codes", align_bytes=64)
        scl = const.tile([P, B], U8, name="scl", align_bytes=64)
        dummy = const.tile([P, 1], F32, name="dummy")
        w_sb = [ring.tile([P, 4 * 512], BF16, name="w_sb", tag="cn", align_bytes=64) for half_ in range(2)]
        gw = [ring.tile([P, 4 * 512], BF16, name="gw", tag="cn", align_bytes=64) for half_ in range(3)]

        xhq, mq, ncq, gq = {}, {}, {}, {}
        eT, zT, thT = {}, {}, {}
        e1q, e2q, fq, nnq, cnq, mnq, sqq, a_t = {}, {}, {}, {}, {}, {}, {}, {}
        quantised, quantised_w = {}, {}

        fills, bankof = [], {}
        jobs, tb_of = [], {}
        state = {"filled": 0, "used": 0, "tpe": 0, "tact": 0, "tlim": 0}

        def pump(ring=NRING):
            while fills and state["filled"] - state["used"] < ring:
                if not fills[0]():
                    break
                fills.pop(0)
                state["filled"] += 1

        def used(ring=NRING):
            state["used"] += 1
            pump(ring)

        def tpump():
            while state["tpe"] < min(len(jobs), state["tlim"]) and state["tpe"] - state["tact"] < 2:
                if not jobs[state["tpe"]][0]():
                    break
                state["tpe"] += 1

        def tjob(ring=NRING):
            state["tlim"] = max(state["tlim"], state["tact"] + 1)
            tpump()
            assert state["tpe"] > state["tact"], "job not ready"
            jobs[state["tact"]][1]()
            state["tact"] += 1
            tpump()
            pump(ring)

        def load_m(q):
            mq[q] = ld.tile([P, QW], BF16, name="mq", tag="m")
            nc.sync.dma_start(out=mq[q][:], in_=mv[:, q * QW : (q + 1) * QW])

        def load_nc(q):
            ncq[q] = ld.tile([P, 2 * QW], BF16, name="ncq", tag="nc")
            nc.sync.dma_start(out=ncq[q][:, 0:QW], in_=nv[:, q * QW : (q + 1) * QW])
            nc.sync.dma_start(out=ncq[q][:, QW : 2 * QW], in_=cv[:, q * QW : (q + 1) * QW])

        def load_xh(q):
            xhq[q] = ld.tile([P, 4 * 512], BF16, name="xhq", tag="xh")
            for side, src in enumerate((xv, hv)):
                nc.sync.dma_start(
                    out=xhq[q][:].rearrange("p (t s d) -> p t s d", t=4, s=2)[:, :, side, :],
                    in_=src[:, q * QW : (q + 1) * QW].rearrange("p (t d) -> p t d", t=4),
                )

        def store(g, q, t):
            nc.sync.dma_start(out=ov[g, :, q * QW : (q + 1) * QW], in_=t[:])

        def add_e1(key, ins_fn, out_fn, eng, ready_fn, after=None):
            def pe():
                if not ready_fn():
                    return False
                tp = ps.tile([P, 512], F32, name="bank_T", tag="T", bufs=2)
                tb_of[key] = tp
                for i, src in enumerate(ins_fn()):
                    nc.tensor.transpose(tp[:, i * P : (i + 1) * P], src, ident32[:])
                return True

            def drain():
                src = tb_of[key][:].rearrange("p (s u c) -> p s c u", s=2, u=2)
                if eng == "act":
                    nc.scalar.copy(out=out_fn(), in_=src)
                else:
                    nc.vector.tensor_copy(out=out_fn(), in_=src)
                if after is not None:
                    after()

            jobs.append((pe, drain))

        def gw_of(blk, nblk):
            t, b0 = {GI: (1, GI), GF: (0, GF), GN: (0, GF), GZ: (2, GZ), GO: (2, GZ)}[blk]
            return gw[t][:, (blk - b0) * 512 : (blk - b0 + nblk) * 512]

        def add_e1_w(k, blk, eng):
            w32 = w_sb[k // 2][:].bitcast(F32)
            gw32 = gw_of(blk, 2).bitcast(F32).rearrange("p (s c u) -> p s c u", s=2, u=2)
            add_e1(
                ("w", k),
                lambda: [w32[:, (2 * (k % 2) + s) * 256 + u : (2 * (k % 2) + s + 1) * 256 : 2] for s in range(2) for u in range(2)],
                lambda: gw32,
                eng,
                lambda: True,
            )

        def add_exit(q, blk, dst, func, bias, scale, tag, bufs, blk2=None):
            key = (tag, q, blk)

            def pe():
                if q not in quantised or blk not in quantised_w or (blk2 is not None and blk2 not in quantised_w):
                    return False
                tbk = ps.tile([P, 512], F32, name="bank_T", tag="T", bufs=2)
                tb_of[key] = tbk
                seq = [blk] if blk2 is None else [blk, blk2]
                for k, bl in enumerate(seq):
                    nc.tensor.matmul_mx(
                        out=tbk[:],
                        lhsT=wc[:, bl * P : (bl + 1) * P].bitcast(FP8X4),
                        lhsT_scale=wscl[:, bl * P : (bl + 1) * P],
                        rhs=codes[:, q * 512 : (q + 1) * 512].bitcast(FP8X4),
                        rhs_scale=scl[:, q * 512 : (q + 1) * 512],
                        start=k == 0,
                        stop=k == len(seq) - 1,
                    )
                return True

            def drain():
                dst[(q, blk % 2)] = gt.tile([P, 512], F32, name=tag, tag=tag + str(blk % 2), bufs=bufs)
                nc.scalar.activation(out=dst[(q, blk % 2)][:], in_=tb_of[key][:], func=func, bias=bias, scale=scale)

            jobs.append((pe, drain))

        def add_exit_e(q):
            for r in range(2):
                add_exit(q, GF + r, eT, ACT.Identity, bd[:, r : r + 1], 1.0, "eT", 2, blk2=GN + r)

        def add_exit_z(q):
            for r in range(2):
                add_exit(q, GZ + r, zT, ACT.Tanh, bcol[:, 4 + r : 5 + r], 1.0, "zT", 2)

        def add_exit_o(q):
            for r in range(2):
                add_exit(q, GO + r, thT, ACT.Tanh, bhalf[:, r : r + 1], 0.5, "thT", 4)

        def quant(q):
            nc.vector.quantize_mx(
                out=codes[:, q * 512 : (q + 1) * 512].bitcast(FP8X4),
                scales=scl[:, q * 512 : (q + 1) * 512],
                in_=gq[q][:],
            )
            quantised[q] = True
            tpump()
            if q > 0:
                pump()

        def quant_w(s0, nblk):
            nc.vector.quantize_mx(
                out=wc[:, s0 * P : (s0 + nblk) * P].bitcast(FP8X4),
                scales=wscl[:, s0 * P : (s0 + nblk) * P],
                in_=gw_of(s0, nblk),
            )
            for bl in range(s0, s0 + nblk):
                quantised_w[bl] = True
            tpump()

        def new_bank(key):
            bankof[key] = ps.tile([P, 512], F32, name="bank_B", tag="B", bufs=NRING)
            return bankof[key]

        def add_x(j):
            q, jj = j // 2, j % 2

            def go():
                if q not in xhq:
                    return False
                bk = new_bank(("X", j))
                xh32 = xhq[q][:].bitcast(F32)
                for tt in range(2):
                    for u in range(2):
                        t = 2 * jj + tt
                        nc.tensor.transpose(bk[:, (2 * tt + u) * P : (2 * tt + u + 1) * P], xh32[:, t * 256 + u : (t + 1) * 256 : 2], ident32[:])
                return True

            fills.append(go)

        def xcopy(j, eng, ring=NRING):
            q, jj = j // 2, j % 2
            if jj == 0:
                gq[q] = grp.tile([P, 4 * 512], BF16, name="g", tag="g", align_bytes=64)
            dst = gq[q][:].bitcast(F32).rearrange("p (t c u) -> p t c u", t=4, u=2)[:, 2 * jj : 2 * jj + 2]
            src = bankof[("X", j)][:].rearrange("p (s u c) -> p s c u", s=2, u=2)
            if eng == "act":
                nc.scalar.copy(out=dst, in_=src)
            else:
                nc.vector.tensor_copy(out=dst, in_=src)
            used(ring)
            if jj == 1 and q + 3 < NQ:
                load_xh(q + 3)

        def add_i(j):
            def go():
                if j // 2 not in quantised or GI not in quantised_w:
                    return False
                bk = new_bank(("I", j))
                for tt in range(2):
                    t = 2 * j + tt
                    nc.tensor.matmul_mx(
                        out=bk[:, tt * DIM : (tt + 1) * DIM],
                        lhsT=codes[:, t * P : (t + 1) * P].bitcast(FP8X4),
                        lhsT_scale=scl[:, t * P : (t + 1) * P],
                        rhs=wc[:, GI * P : (GI + 2) * P].bitcast(FP8X4),
                        rhs_scale=wscl[:, GI * P : (GI + 2) * P],
                        start=True,
                        stop=True,
                    )
                return True

            fills.append(go)

        def back(bk, src, j, plus_m):
            q, jj = j // 2, j % 2
            if plus_m:
                nc.tensor.matmul(out=bk[:], lhsT=identb[:], rhs=mq[q][:, jj * PW : (jj + 1) * PW], start=True, stop=False)
            for tt in range(2):
                for r in range(2):
                    o = bk[:, tt * DIM + r * P : tt * DIM + (r + 1) * P]
                    i = src[(q, r)][:, (2 * jj + tt) * P : (2 * jj + tt + 1) * P]
                    if plus_m:
                        nc.tensor.matmul(out=o, lhsT=i, rhs=ident32[:], is_transpose=True, start=False, stop=(tt == 1 and r == 1))
                    else:
                        nc.tensor.transpose(o, i, ident32[:])

        def add_back(kind, src, j):
            def go():
                if (j // 2, 0) not in src or (j // 2, 1) not in src:
                    return False
                back(new_bank((kind, j)), src, j, False)
                return True

            fills.append(go)

        def fill_e(j):
            bankof[("E", j)] = ps.tile([P, 512], F32, name="bank_E", tag="E", bufs=2)
            back(bankof[("E", j)], eT, j, True)

        def half(t, j):
            return t[:, (j % 2) * PW : (j % 2 + 1) * PW]

        def v_a(j):
            a_t[j] = wk.tile([P, PW], F32, name="a", tag="a")
            nc.vector.tensor_tensor(out=a_t[j][:], in0=bankof[("I", j)][:], in1=bib[:], op=ALU.add)
            used()

        def v_mn(j):
            q = j // 2
            if j % 2 == 0:
                mnq[q] = ost.tile([P, QW], F32, name="mn", tag="mn")
            nc.vector.scalar_tensor_tensor(out=half(mnq[q], j), in0=bankof[("E", j)][:], scalar=0.0, in1=a_t[j][:], op0=ALU.max, op1=ALU.add)
            if j % 2 == 1:
                store(3, q, mnq[q])

        def s_exps(j):
            q = j // 2
            if j % 2 == 0:
                e1q[q] = wk.tile([P, QW], F32, name="e1", tag="e1", bufs=3)
                e2q[q] = wk.tile([P, QW], F32, name="e2", tag="e2")
            nc.scalar.activation(out=half(e2q[q], j), in_=bankof[("E", j)][:], func=ACT.Exp, scale=1.0)
            nc.scalar.activation(out=half(e1q[q], j), in_=bankof[("E", j)][:], func=ACT.Exp, scale=-1.0)

        def v_f(q):
            fq[q] = wk.tile([P, 2 * QW], F32, name="fnc", tag="fnc", bufs=1)
            nc.vector.scalar_tensor_tensor(
                out=fq[q][:].rearrange("p (s d) -> p s d", s=2),
                in0=e2q[q][:].unsqueeze(1).to_broadcast([P, 2, QW]),
                scalar=1.0,
                in1=ncq[q][:].rearrange("p (s d) -> p s d", s=2),
                op0=ALU.min,
                op1=ALU.mult,
            )

        def v_nn(q):
            nnq[q] = ring.tile([P, QW], F32, name="nn", tag="nn")
            nc.vector.scalar_tensor_tensor(out=nnq[q][:], in0=e1q[q][:], scalar=1.0, in1=fq[q][:, 0:QW], op0=ALU.min, op1=ALU.add)
            store(2, q, nnq[q])

        def s_sq(q):
            sqq[q] = ring.tile([P, QW], F32, name="sq", tag="sq")
            nc.scalar.activation(out=sqq[q][:], in_=nnq[q][:], func=ACT.Square, bias=epsc[:], scale=1.0)

        def v_iz(j):
            e1h = half(e1q[j // 2], j)
            nc.vector.scalar_tensor_tensor(out=e1h, in0=e1h, scalar=1.0, in1=bankof[("Z", j)][:], op0=ALU.min, op1=ALU.mult)
            used()

        def cn(j):
            q = j // 2
            if j % 2 == 0:
                cnq[q] = ring.tile([P, QW], F32, name="cn", tag="cn", align_bytes=64)
            eng = nc.gpsimd if q in CN_GPSIMD else nc.vector
            eng.tensor_tensor(out=half(cnq[q], j), in0=half(e1q[q], j), in1=half(fq[q][:, QW : 2 * QW], j), op=ALU.add)
            if j % 2 == 1:
                store(1, q, cnq[q])

        def v_p(q):
            nc.vector.scalar_tensor_tensor(out=nnq[q][:], in0=nnq[q][:], scalar=EPS, in1=cnq[q][:], op0=ALU.add, op1=ALU.mult)

        def s_ln(q):
            nc.scalar.activation(out=sqq[q][:], in_=sqq[q][:], func=ACT.Ln, scale=2.0)

        def s_r2(q):
            nc.scalar.activation(out=sqq[q][:], in_=sqq[q][:], func=ACT.Exp, scale=-1.0)

        def p2(q):
            eng = nc.gpsimd if q in P2_GPSIMD else nc.vector
            eng.tensor_tensor(out=sqq[q][:], in0=nnq[q][:], in1=sqq[q][:], op=ALU.mult)

        def v_h(j):
            q = j // 2
            nc.vector.scalar_tensor_tensor(out=half(sqq[q], j), in0=bankof[("TH", j)][:], scalar=1.0, in1=half(sqq[q], j), op0=ALU.add, op1=ALU.mult)
            used()
            if q == NQ - 1:
                nc.sync.dma_start(out=ov[0, :, j * PW : (j + 1) * PW], in_=half(sqq[q], j))
            elif j % 2 == 1:
                store(0, q, sqq[q])

        add_e1_w(0, GI, "act")
        add_e1_w(1, GF, "dve")
        add_e1_w(2, GZ, "act")
        add_e1_w(3, GO, "act")
        add_exit_e(0)
        plan = {}
        for it in range(NQ + 1):
            todo = ""
            if it + 1 < NQ:
                add_exit_e(it + 1)
                todo += "ee"
            if it < NQ:
                add_exit_z(it)
                todo += "zz"
            for hq in O_AT.get(it, []):
                add_exit_o(hq)
                todo += "oo"
            plan[it] = list(todo)
        for q in range(3):
            add_x(2 * q)
            add_x(2 * q + 1)
        for q in range(4, NQ):
            add_exit_o(q)
        for it in range(NQ + 1):
            if 1 <= it <= NQ:
                add_back("Z", zT, 2 * (it - 1))
                add_back("Z", zT, 2 * (it - 1) + 1)
            if it < NQ:
                add_i(2 * it)
                add_i(2 * it + 1)
            if it + 3 < NQ:
                add_x(2 * (it + 3))
                add_x(2 * (it + 3) + 1)
        for q in range(NQ):
            add_back("TH", thT, 2 * q)
            add_back("TH", thT, 2 * q + 1)

        def load_w(k, wg):
            nc.sync.dma_start(
                out=w_sb[k // 2][:, 2 * (k % 2) * 512 : (2 * (k % 2) + 2) * 512].rearrange("p (r k) -> p r k", r=2),
                in_=wg.rearrange("(r p) k -> p r k", p=P),
            )

        nc.vector.memset(brow[:], 0.0)
        nc.vector.memset(epsc[:], EPS)
        make_identity(nc, ident32[:])
        load_w(0, W_i)
        load_w(1, W_f)
        load_xh(0)
        for g, bg in enumerate((b_i, b_f, b_z, b_o)):
            nc.scalar.dma_start(out=brow[2 * g : 2 * g + 2, :], in_=bg.rearrange("(r c) -> r c", r=2))
        nc.scalar.activation(out=dummy[:], in_=epsc[:], func=ACT.Exp)
        load_m(0)
        load_w(2, W_z)
        load_w(3, W_o)
        load_xh(1)
        load_nc(0)
        load_xh(2)
        load_m(1)

        nc.vector.tensor_copy(out=identb[:], in_=ident32[:])
        state["tlim"] = 1
        tpump()
        tb = ps.tile([P, 512], F32, name="bank_E", tag="E", bufs=2)
        tbb = tb[:].bitcast(BF16)
        nc.tensor.transpose(tbb[:, 0:P], brow[:], identb[:])
        for r in range(2):
            nc.tensor.matmul(out=tb[:, DIM + r * P : DIM + (r + 1) * P], lhsT=identb[:, r : r + 1].to_broadcast([P, P]), rhs=brow[:], start=True, stop=True)
        nc.vector.tensor_copy(out=bcol[:], in_=tbb[:, 0:10])
        nc.vector.tensor_tensor(out=bd[:], in0=bcol[:, 2:4], in1=bcol[:, 0:2], op=ALU.subtract)
        nc.vector.tensor_scalar(out=bhalf[:], in0=bcol[:, 6:8], scalar1=0.5, scalar2=None, op0=ALU.mult)
        for r in range(2):
            nc.vector.tensor_copy(out=bib[:, r * DIM : (r + 1) * DIM], in_=tb[:, DIM : 2 * DIM])
        state["tlim"] = 2
        tpump()
        pump(2)
        tjob(0)
        tjob(0)
        nc.vector.tensor_scalar(out=gw_of(GN, 2), in0=gw_of(GI, 2), scalar1=-1.0, scalar2=None, op0=ALU.mult)
        quant_w(GF, 4)
        xcopy(0, "act", 0)
        xcopy(1, "dve", 0)
        state["tlim"] = 6
        tpump()
        tjob(0)
        tjob(0)
        quant(0)
        quant_w(GI, 2)
        quant_w(GZ, 4)
        pump(2)
        tjob(2)
        tjob(2)
        fill_e(0)
        fill_e(1)
        pump()
        s_exps(0)
        s_exps(1)
        xcopy(2, "dve", 0)
        xcopy(3, "dve", 0)
        state["tlim"] = 8
        quant(1)
        xcopy(4, "dve")
        xcopy(5, "dve")

        for it in range(NQ + 1):
            qa = it if it < NQ else None
            qk = it - 1 if 1 <= it <= NQ else None
            if it + 2 < NQ:
                load_m(it + 2)
            if it + 1 < NQ:
                load_nc(it + 1)
            todo = plan[it]

            def act_jobs(kinds, ahead=0):
                k = 0
                while k < len(todo) and todo[k] in kinds:
                    k += 1
                state["tlim"] = state["tact"] + k + ahead
                for i in range(k):
                    todo.pop(0)
                    tjob()

            if qk is not None:
                v_f(qk)
            act_jobs("e")
            if qk == NQ - 1:
                v_nn(qk)
                s_sq(qk)
                s_ln(qk)

            act_jobs("z")
            if it == NQ - 1:
                for q in range(NQ - 2):
                    s_ln(q)
            if qk is not None and qk < NQ - 1:
                v_nn(qk)
            if 2 <= it + 2 < NQ:
                quant(it + 2)
            if qk is not None and qk < NQ - 1:
                s_sq(qk)
            if it == NQ - 1:
                s_ln(NQ - 2)
            if qk is not None:
                v_iz(2 * qk)
                v_iz(2 * qk + 1)
                cn(2 * qk)
                cn(2 * qk + 1)
            act_jobs("o")
            if qa is not None:
                v_a(2 * qa)
                v_a(2 * qa + 1)
                v_mn(2 * qa)
                v_mn(2 * qa + 1)
            if it + 1 < NQ:
                fill_e(2 * (it + 1))
                fill_e(2 * (it + 1) + 1)
            if it + 3 < NQ:
                for j in (2 * (it + 3), 2 * (it + 3) + 1):
                    xcopy(j, "act" if j in X_SCALAR else "dve")
            if it + 1 < NQ:
                s_exps(2 * (it + 1))
                s_exps(2 * (it + 1) + 1)
        for q in range(NQ):
            v_p(q)

        def exit_o(q):
            tjob()
            tjob()

        state["tlim"] = len(jobs)
        tpump()
        s_r2(0)
        s_r2(1)
        p2(0)
        p2(1)
        for q in range(0, NQ, 2):
            if q + 2 < NQ:
                s_r2(q + 2)
                s_r2(q + 3)
                p2(q + 2)
                exit_o(4 + q // 2)
            v_h(2 * q)
            v_h(2 * q + 1)
            v_h(2 * q + 2)
            v_h(2 * q + 3)
            if q == 4:
                exit_o(7)
            if q + 2 < NQ:
                p2(q + 3)
